import numpy as np
import ml_dtypes


def mxq(x, axis, fmt="e4m3"):
    dtype, down = {"e4m3": (ml_dtypes.float8_e4m3fn, 7), "e5m2": (ml_dtypes.float8_e5m2, 14)}[fmt]
    v = np.moveaxis(np.asarray(x, np.float32).astype(ml_dtypes.bfloat16).astype(np.float64), axis, -1)
    blocks = v.reshape(v.shape[:-1] + (-1, 32))
    amax = np.abs(blocks).max(-1, keepdims=True)
    byte = np.maximum(np.where(amax > 0, np.frexp(amax)[1] - 1 + 127, 0) - down, 1)
    scale = np.exp2(byte - 127.0)
    codes = (blocks / scale).astype(np.float32).astype(dtype).astype(np.float64)
    return np.moveaxis((codes * scale).reshape(v.shape), -1, axis)


WIDE = False


def mx_kscale(k):
    if not WIDE:
        return np.ones(k)
    levels = np.array([10, -10, 5, -5, 0])
    a = np.random.permutation(np.resize(levels, k // 512 * 4)).reshape(k // 512, 4)
    idx = np.arange(k)
    return np.exp2(a[idx // 512, idx % 128 // 32])


BF16 = ml_dtypes.bfloat16


def bf(x):
    return np.asarray(x, np.float32).astype(BF16)


def f64(x):
    return np.asarray(x).astype(np.float64)


N, D_IN, D_HID, D_OUT = 256, 128, 128, 384


def hamilton_Wq(Wr, Wi, Wj, Wk, xr, xi, xj, xk):
    x_cat = np.concatenate([xr, xi, xj, xk], axis=-1)
    n_in = Wr.shape[1]
    Wq = mxq(np.concatenate([Wr, Wi, Wj, Wk], axis=1), 1, "e4m3")
    Wr, Wi, Wj, Wk = Wq[:, :n_in], Wq[:, n_in:2 * n_in], Wq[:, 2 * n_in:3 * n_in], Wq[:, 3 * n_in:]
    W_block = np.concatenate([
        np.concatenate([Wr, Wi, Wj, Wk], axis=0),
        np.concatenate([-Wi, Wr, -Wk, Wj], axis=0),
        np.concatenate([-Wj, Wk, Wr, -Wi], axis=0),
        np.concatenate([-Wk, -Wj, Wi, Wr], axis=0),
    ], axis=1)
    h = mxq(x_cat, 1, "e4m3") @ W_block.T
    out = Wr.shape[0]
    return h[:, :out], h[:, out:2 * out], h[:, 2 * out:3 * out], h[:, 3 * out:]


def setup_inputs():
    s = mx_kscale(4 * D_IN)[:D_IN]
    t = mx_kscale(4 * D_HID)[:D_HID]
    inp = {}
    for c in "rijk":
        inp["q_" + c] = bf(np.random.standard_normal((N, D_IN)) * s)
    for c in "rijk":
        inp["W1_" + c] = bf(np.random.standard_normal((D_HID, D_IN)) * 0.5 / np.sqrt(D_IN) / s[None, :] * t[:, None])
    for c in "rijk":
        inp["b1_" + c] = bf(((0.0 if c == "r" else 0.2) + 0.1 * np.random.standard_normal(D_HID)) * t)
    for c in "rijk":
        inp["W2_" + c] = bf(np.random.standard_normal((D_OUT, D_HID)) * 0.7 / np.sqrt(D_HID) / t[None, :])
    for c in "rijk":
        inp["b2_" + c] = bf((0.0 if c == "r" else 0.2) + 0.1 * np.random.standard_normal(D_OUT))
    return inp


def reference(q_r, q_i, q_j, q_k,
              W1_r, W1_i, W1_j, W1_k, b1_r, b1_i, b1_j, b1_k,
              W2_r, W2_i, W2_j, W2_k, b2_r, b2_i, b2_j, b2_k):
    hr, hi, hj, hk = hamilton_Wq(f64(W1_r), f64(W1_i), f64(W1_j), f64(W1_k), f64(q_r), f64(q_i), f64(q_j), f64(q_k))
    hr = np.maximum(hr + f64(b1_r), 0.0)
    hi = np.maximum(hi + f64(b1_i), 0.0)
    hj = np.maximum(hj + f64(b1_j), 0.0)
    hk = np.maximum(hk + f64(b1_k), 0.0)
    or_, oi, oj, ok = hamilton_Wq(f64(W2_r), f64(W2_i), f64(W2_j), f64(W2_k), hr, hi, hj, hk)
    return (or_ + f64(b2_r), oi + f64(b2_i), oj + f64(b2_j), ok + f64(b2_k))

@@ -1,0 +1,222 @@
+import concourse.mybir as mybir
+from concourse.masks import make_identity
+
+F32 = mybir.dt.float32
+BF16 = mybir.dt.bfloat16
+U32 = mybir.dt.uint32
+U8 = mybir.dt.uint8
+FP8X4 = mybir.dt.float8_e4m3fn_x4
+ALU = mybir.AluOpType
+ACT = mybir.ActivationFunctionType
+
+P = 128
+PACK = 4
+COMPONENTS = 4
+ROWS, FEATURES, D_OUT = 256, 128, 384
+ROW_HALVES = ROWS // P
+WORDS = FEATURES // 2
+WINDOW_WORDS = COMPONENTS * WORDS
+SLOTS = 12
+R, I, J, K = 0, 1, 2, 3
+FIRST_SLOT = {J: 0, R: 2, I: 6, K: 8}
+RAW_SLOT = {J: 0, K: 1, R: 2, I: 3}
+ORDER = (J, R, I, K)
+OUT_TILES = D_OUT // P
+COLUMNS_2 = COMPONENTS * D_OUT
+CHUNK = 256
+FLOPS = 2 * ROWS * 512 * (COMPONENTS * FEATURES + COLUMNS_2)
+
+
+def fill_signed_slots(nc, slots):
+    nc.vector.tensor_scalar_mul(out=slots[:, :, 4:6, :], in0=slots[:, :, 0:2, :], scalar1=-1.0)
+    nc.vector.tensor_scalar_mul(out=slots[:, :, 7:11:3, :], in0=slots[:, :, 2:4, :], scalar1=-1.0)
+    nc.vector.tensor_copy(out=slots[:, :, 8:10, :], in_=slots[:, :, 1:5:3, :])
+    nc.vector.tensor_copy(out=slots[:, :, 6, :], in_=slots[:, :, 3, :])
+    nc.vector.tensor_copy(out=slots[:, :, 11, :], in_=slots[:, :, 2, :])
+
+
+def transpose_windows(nc, psum, identity, windows):
+    transposed = psum.tile([P, len(windows), 2, P], F32, tag="transposed")
+    for n, window in enumerate(windows):
+        halves = window.rearrange("p (m u) -> p u m", u=2)
+        for u in range(2):
+            nc.tensor.transpose(transposed[:, n, u, :], halves[:, u, :], identity)
+    return transposed
+
+
+def tile_qmlp_s_kernel(
+    tc,
+    q_r, q_i, q_j, q_k,
+    W1_r, W1_i, W1_j, W1_k,
+    b1_r, b1_i, b1_j, b1_k,
+    W2_r, W2_i, W2_j, W2_k,
+    b2_r, b2_i, b2_j, b2_k,
+    out_0, out_1, out_2, out_3,
+):
+    nc = tc.nc
+    q = (q_r, q_i, q_j, q_k)
+    W1 = (W1_r, W1_i, W1_j, W1_k)
+    b1 = (b1_r, b1_i, b1_j, b1_k)
+    W2 = (W2_r, W2_i, W2_j, W2_k)
+    b2 = (b2_r, b2_i, b2_j, b2_k)
+    outs = (out_0, out_1, out_2, out_3)
+
+    with (
+        tc.tile_pool(name="keep", bufs=1) as keep,
+        tc.psum_pool(name="psum_t", bufs=4) as psum_t,
+        tc.psum_pool(name="psum_mx", bufs=4) as psum_mx,
+    ):
+        identity = keep.tile([P, P], F32)
+        make_identity(nc, identity[:])
+        sign = keep.tile([P, 1], F32)
+        nc.vector.memset(sign[:], 1.0)
+        nc.vector.memset(sign[32 * I : 32 * I + 32, :], -1.0)
+        table_warmer = keep.tile([P, 1], F32)
+        nc.scalar.activation(out=table_warmer[:], in_=sign[:], func=ACT.Relu)
+
+        q_sb = keep.tile([P, ROW_HALVES * COMPONENTS * FEATURES], BF16)
+        q_view = q_sb[:].rearrange("p (h c f) -> p h c f", h=ROW_HALVES, c=COMPONENTS)
+        w1_sb = keep.tile([P, SLOTS * FEATURES], BF16)
+        w1_slots = w1_sb[:].rearrange("p (t s f) -> p t s f", t=1, s=SLOTS)
+        w2_sb = keep.tile([P, OUT_TILES * SLOTS * FEATURES], BF16)
+        w2_slots = w2_sb[:].rearrange("p (t s f) -> p t s f", t=OUT_TILES, s=SLOTS)
+        b1_sb = keep.tile([P, PACK], BF16)
+        b2_sb = keep.tile([P, COLUMNS_2], BF16)
+
+        for c in (I, R, J, K):
+            nc.sync.dma_start(out=q_view[:, :, c, :], in_=q[c].rearrange("(p h) f -> p h f", h=ROW_HALVES))
+        for c in (J, K, R, I):
+            nc.scalar.dma_start(out=w1_slots[:, 0, RAW_SLOT[c], :], in_=W1[c])
+        for c in (J, K, R, I):
+            nc.sync.dma_start(
+                out=w2_slots[:, :, RAW_SLOT[c], :], in_=W2[c].rearrange("(t p) f -> p t f", p=P)
+            )
+        for c in range(COMPONENTS):
+            nc.scalar.dma_start(out=b1_sb[32 * c : 32 * c + 32, :], in_=b1[c].rearrange("(m t) -> m t", t=PACK))
+        for n, c in enumerate(ORDER):
+            nc.gpsimd.dma_start(out=b2_sb[:, n * D_OUT : (n + 1) * D_OUT], in_=b2[c].partition_broadcast(P))
+
+        nc.vector.tensor_scalar_mul(out=q_view[:, :, I, :], in0=q_view[:, :, I, :], scalar1=-1.0)
+        fill_signed_slots(nc, w1_slots)
+
+        q_words = q_sb[:].bitcast(F32)
+        x_grouped = keep.tile([P, ROWS * PACK], BF16, align_bytes=64)
+        x_words = x_grouped[:].bitcast(F32).rearrange("p (h r u) -> p h r u", h=ROW_HALVES, u=2)
+        x_codes = keep.tile([P, ROWS], U32, align_bytes=64)
+        x_scales = keep.tile([P, ROWS], U8, align_bytes=64)
+        for half in range(ROW_HALVES):
+            window = q_words[:, half * WINDOW_WORDS : (half + 1) * WINDOW_WORDS]
+            transposed = transpose_windows(nc, psum_t, identity[:], [window])
+            source = transposed[:, 0, :, :].rearrange("p u r -> p r u")
+            if half % 2 == 0:
+                nc.scalar.copy(out=x_words[:, half, :, :], in_=source)
+            else:
+                nc.vector.tensor_copy(out=x_words[:, half, :, :], in_=source)
+        nc.vector.quantize_mx(out=x_codes[:].bitcast(FP8X4), scales=x_scales[:], in_=x_grouped[:])
+
+        w1_words = w1_sb[:].bitcast(F32)
+        w1_grouped = keep.tile([P, COMPONENTS * FEATURES * PACK], BF16, align_bytes=64)
+        w1_grouped_words = w1_grouped[:].bitcast(F32).rearrange(
+            "p (t c m u) -> p t c m u", t=PACK, c=COMPONENTS, u=2
+        )
+        w1_codes = keep.tile([P, COMPONENTS * FEATURES], U32, align_bytes=64)
+        w1_scales = keep.tile([P, COMPONENTS * FEATURES], U8, align_bytes=64)
+        for n, c in enumerate(ORDER):
+            window = w1_words[:, FIRST_SLOT[c] * WORDS : FIRST_SLOT[c] * WORDS + WINDOW_WORDS]
+            transposed = transpose_windows(nc, psum_t, identity[:], [window])
+            source = transposed[:, 0, :, :].rearrange("p u (m t) -> p t m u", t=PACK)
+            if n % 2 == 0:
+                nc.scalar.copy(out=w1_grouped_words[:, :, c, :, :], in_=source)
+            else:
+                nc.vector.tensor_copy(out=w1_grouped_words[:, :, c, :, :], in_=source)
+        for t in range(PACK):
+            cols = slice(t * P, (t + 1) * P)
+            nc.vector.quantize_mx(
+                out=w1_codes[:, cols].bitcast(FP8X4),
+                scales=w1_scales[:, cols],
+                in_=w1_grouped[:, t * P * PACK : (t + 1) * P * PACK],
+            )
+
+        h_planes = keep.tile([P, PACK, ROWS], BF16)
+        for t in range(PACK):
+            cols = slice(t * P, (t + 1) * P)
+            hidden = psum_mx.tile([P, ROWS], F32, tag="mx")
+            nc.tensor.matmul_mx(
+                out=hidden[:],
+                lhsT=w1_codes[:, cols].bitcast(FP8X4),
+                lhsT_scale=w1_scales[:, cols],
+                rhs=x_codes[:].bitcast(FP8X4),
+                rhs_scale=x_scales[:],
+                start=True,
+                stop=True,
+            )
+            if t % 2 == 0:
+                nc.scalar.activation(out=h_planes[:, t, :], in_=hidden[:], func=ACT.Relu, bias=b1_sb[:, t : t + 1])
+            else:
+                nc.vector.tensor_scalar(
+                    out=h_planes[:, t, :], in0=hidden[:], scalar1=b1_sb[:, t : t + 1], scalar2=0.0,
+                    op0=ALU.add, op1=ALU.max,
+                )
+        h_grouped = keep.tile([P, ROWS * PACK], BF16, align_bytes=64)
+        h_codes = keep.tile([P, ROWS], U32, align_bytes=64)
+        h_scales = keep.tile([P, ROWS], U8, align_bytes=64)
+        for half in range(ROW_HALVES):
+            rows = slice(half * P, (half + 1) * P)
+            grouped = h_grouped[:, half * P * PACK : (half + 1) * P * PACK]
+            nc.vector.tensor_scalar_mul(
+                out=grouped.rearrange("p (r t) -> p r t", t=PACK),
+                in0=h_planes[:, :, rows].rearrange("p t r -> p r t"),
+                scalar1=sign[:, 0:1],
+            )
+            nc.vector.quantize_mx(out=h_codes[:, rows].bitcast(FP8X4), scales=h_scales[:, rows], in_=grouped)
+
+        fill_signed_slots(nc, w2_slots)
+        w2_words = w2_sb[:].bitcast(F32).rearrange("p (t w) -> p t w", t=OUT_TILES)
+        windows = [
+            w2_words[:, tile, FIRST_SLOT[c] * WORDS : FIRST_SLOT[c] * WORDS + WINDOW_WORDS]
+            for c in ORDER
+            for tile in range(OUT_TILES)
+        ]
+        w2_grouped = keep.tile([P, COLUMNS_2 * PACK], BF16, align_bytes=64)
+        w2_grouped_words = w2_grouped[:].bitcast(F32).rearrange("p (n o u) -> p n o u", o=P, u=2)
+        w2_codes = keep.tile([P, COLUMNS_2], U32, align_bytes=64)
+        w2_scales = keep.tile([P, COLUMNS_2], U8, align_bytes=64)
+        result = keep.tile([P, ROW_HALVES, COLUMNS_2], F32)
+        per_chunk = CHUNK // P
+        for chunk in range(COLUMNS_2 // CHUNK):
+            cols = slice(chunk * CHUNK, (chunk + 1) * CHUNK)
+            first = chunk * per_chunk
+            transposed = transpose_windows(nc, psum_t, identity[:], windows[first : first + per_chunk])
+            nc.scalar.copy(
+                out=w2_grouped_words[:, first : first + per_chunk, :, :],
+                in_=transposed[:].rearrange("p n u o -> p n o u"),
+            )
+            nc.vector.quantize_mx(
+                out=w2_codes[:, cols].bitcast(FP8X4),
+                scales=w2_scales[:, cols],
+                in_=w2_grouped[:, chunk * CHUNK * PACK : (chunk + 1) * CHUNK * PACK],
+            )
+            product = psum_mx.tile([P, ROW_HALVES, CHUNK], F32, tag="mx")
+            for half in range(ROW_HALVES):
+                rows = slice(half * P, (half + 1) * P)
+                nc.tensor.matmul_mx(
+                    out=product[:, half, :],
+                    lhsT=h_codes[:, rows].bitcast(FP8X4),
+                    lhsT_scale=h_scales[:, rows],
+                    rhs=w2_codes[:, cols].bitcast(FP8X4),
+                    rhs_scale=w2_scales[:, cols],
+                    start=True,
+                    stop=True,
+                )
+            nc.vector.tensor_tensor(
+                out=result[:, :, cols],
+                in0=product[:],
+                in1=b2_sb[:, cols].unsqueeze(1).to_broadcast([P, ROW_HALVES, CHUNK]),
+                op=ALU.add,
+            )
+            for n, c in enumerate(ORDER):
+                if ((n + 1) * D_OUT - 1) // CHUNK == chunk:
+                    nc.sync.dma_start(
+                        out=outs[c].rearrange("(p h) o -> p h o", h=ROW_HALVES),
+                        in_=result[:, :, n * D_OUT : (n + 1) * D_OUT],
+                    )

@@ -23,6 +23,7 @@ RAW_SLOT = {J: 0, K: 1, R: 2, I: 3}
 ORDER = (J, R, I, K)
 OUT_TILES = D_OUT // P
 COLUMNS_2 = COMPONENTS * D_OUT
+BANK = 512
 CHUNK = 256
 FLOPS = 2 * ROWS * 512 * (COMPONENTS * FEATURES + COLUMNS_2)
 
@@ -81,7 +82,10 @@ def tile_qmlp_s_kernel(
         w2_sb = keep.tile([P, OUT_TILES * SLOTS * FEATURES], BF16)
         w2_slots = w2_sb[:].rearrange("p (t s f) -> p t s f", t=OUT_TILES, s=SLOTS)
         b1_sb = keep.tile([P, PACK], BF16)
-        b2_sb = keep.tile([P, COLUMNS_2], BF16)
+        b2_rows = keep.tile([P, COLUMNS_2], BF16)
+        nc.vector.memset(b2_rows[:].bitcast(mybir.dt.int32), 0)
+        ones = keep.tile([P, P], BF16)
+        nc.vector.memset(ones[:], 1.0)
 
         for c in (I, R, J, K):
             nc.sync.dma_start(out=q_view[:, :, c, :], in_=q[c].rearrange("(p h) f -> p h f", h=ROW_HALVES))
@@ -94,7 +98,7 @@ def tile_qmlp_s_kernel(
         for c in range(COMPONENTS):
             nc.scalar.dma_start(out=b1_sb[32 * c : 32 * c + 32, :], in_=b1[c].rearrange("(m t) -> m t", t=PACK))
         for n, c in enumerate(ORDER):
-            nc.gpsimd.dma_start(out=b2_sb[:, n * D_OUT : (n + 1) * D_OUT], in_=b2[c].partition_broadcast(P))
+            nc.gpsimd.dma_start(out=b2_rows[0:1, n * D_OUT : (n + 1) * D_OUT], in_=b2[c].unsqueeze(0))
 
         nc.vector.tensor_scalar_mul(out=q_view[:, :, I, :], in0=q_view[:, :, I, :], scalar1=-1.0)
         fill_signed_slots(nc, w1_slots)
@@ -136,6 +140,13 @@ def tile_qmlp_s_kernel(
                 scales=w1_scales[:, cols],
                 in_=w1_grouped[:, t * P * PACK : (t + 1) * P * PACK],
             )
+
+        b2_sb = keep.tile([P, COLUMNS_2], F32)
+        for n in range(COLUMNS_2 // BANK):
+            cols = slice(n * BANK, (n + 1) * BANK)
+            spread = psum_mx.tile([P, BANK], F32, tag="mx")
+            nc.tensor.matmul(out=spread[:], lhsT=ones[:], rhs=b2_rows[:, cols], start=True, stop=True)
+            nc.scalar.copy(out=b2_sb[:, cols], in_=spread[:])
 
         h_planes = keep.tile([P, PACK, ROWS], BF16)
         for t in range(PACK):

@@ -25,15 +25,17 @@ OUT_TILES = D_OUT // P
 COLUMNS_2 = COMPONENTS * D_OUT
 BANK = 512
 CHUNK = 256
+CHUNKS = COLUMNS_2 // CHUNK
+ROUND = 2
 FLOPS = 2 * ROWS * 512 * (COMPONENTS * FEATURES + COLUMNS_2)
 
 
-def fill_signed_slots(nc, slots):
+def fill_signed_slots(nc, slots, copy):
     nc.vector.tensor_scalar_mul(out=slots[:, :, 4:6, :], in0=slots[:, :, 0:2, :], scalar1=-1.0)
     nc.vector.tensor_scalar_mul(out=slots[:, :, 7:11:3, :], in0=slots[:, :, 2:4, :], scalar1=-1.0)
-    nc.vector.tensor_copy(out=slots[:, :, 8:10, :], in_=slots[:, :, 1:5:3, :])
-    nc.vector.tensor_copy(out=slots[:, :, 6, :], in_=slots[:, :, 3, :])
-    nc.vector.tensor_copy(out=slots[:, :, 11, :], in_=slots[:, :, 2, :])
+    copy(slots[:, :, 6, :], slots[:, :, 3, :])
+    copy(slots[:, :, 8:10, :], slots[:, :, 1:5:3, :])
+    copy(slots[:, :, 11, :], slots[:, :, 2, :])
 
 
 def transpose_windows(nc, psum, identity, windows):
@@ -66,14 +68,18 @@ def tile_qmlp_s_kernel(
         tc.tile_pool(name="keep", bufs=1) as keep,
         tc.psum_pool(name="psum_t", bufs=4) as psum_t,
         tc.psum_pool(name="psum_mx", bufs=4) as psum_mx,
+        tc.manual_schedule(),
     ):
         identity = keep.tile([P, P], F32)
-        make_identity(nc, identity[:])
+        nc.vector.memset(identity[:], 0.0)
+        make_identity(nc, identity[:], nomemset=True)
         sign = keep.tile([P, 1], F32)
         nc.vector.memset(sign[:], 1.0)
         nc.vector.memset(sign[32 * I : 32 * I + 32, :], -1.0)
-        table_warmer = keep.tile([P, 1], F32)
-        nc.scalar.activation(out=table_warmer[:], in_=sign[:], func=ACT.Relu)
+        b2_rows = keep.tile([P, COLUMNS_2], BF16)
+        nc.vector.memset(b2_rows[:].bitcast(mybir.dt.int32), 0)
+        ones = keep.tile([P, P], BF16)
+        nc.vector.memset(ones[:], 1.0)
 
         q_sb = keep.tile([P, ROW_HALVES * COMPONENTS * FEATURES], BF16)
         q_view = q_sb[:].rearrange("p (h c f) -> p h c f", h=ROW_HALVES, c=COMPONENTS)
@@ -82,26 +88,30 @@ def tile_qmlp_s_kernel(
         w2_sb = keep.tile([P, OUT_TILES * SLOTS * FEATURES], BF16)
         w2_slots = w2_sb[:].rearrange("p (t s f) -> p t s f", t=OUT_TILES, s=SLOTS)
         b1_sb = keep.tile([P, PACK], BF16)
-        b2_rows = keep.tile([P, COLUMNS_2], BF16)
-        nc.vector.memset(b2_rows[:].bitcast(mybir.dt.int32), 0)
-        ones = keep.tile([P, P], BF16)
-        nc.vector.memset(ones[:], 1.0)
 
         for c in (I, R, J, K):
             nc.sync.dma_start(out=q_view[:, :, c, :], in_=q[c].rearrange("(p h) f -> p h f", h=ROW_HALVES))
         for c in (J, K, R, I):
             nc.scalar.dma_start(out=w1_slots[:, 0, RAW_SLOT[c], :], in_=W1[c])
+        for n, c in enumerate(ORDER):
+            nc.gpsimd.dma_start(out=b2_rows[0:1, n * D_OUT : (n + 1) * D_OUT], in_=b2[c].unsqueeze(0))
+        table_warmer = keep.tile([P, 1], F32)
+        nc.scalar.activation(out=table_warmer[:], in_=sign[:], func=ACT.Relu)
         for c in (J, K, R, I):
             nc.sync.dma_start(
                 out=w2_slots[:, :, RAW_SLOT[c], :], in_=W2[c].rearrange("(t p) f -> p t f", p=P)
             )
         for c in range(COMPONENTS):
             nc.scalar.dma_start(out=b1_sb[32 * c : 32 * c + 32, :], in_=b1[c].rearrange("(m t) -> m t", t=PACK))
-        for n, c in enumerate(ORDER):
-            nc.gpsimd.dma_start(out=b2_rows[0:1, n * D_OUT : (n + 1) * D_OUT], in_=b2[c].unsqueeze(0))
+
+        def leave_psum(piece, out, in_):
+            if piece % 2 == 0:
+                nc.vector.tensor_copy(out=out, in_=in_)
+            else:
+                nc.scalar.copy(out=out, in_=in_)
 
         nc.vector.tensor_scalar_mul(out=q_view[:, :, I, :], in0=q_view[:, :, I, :], scalar1=-1.0)
-        fill_signed_slots(nc, w1_slots)
+        fill_signed_slots(nc, w1_slots, lambda out, in_: nc.vector.tensor_copy(out=out, in_=in_))
 
         q_words = q_sb[:].bitcast(F32)
         x_grouped = keep.tile([P, ROWS * PACK], BF16, align_bytes=64)
@@ -111,11 +121,7 @@ def tile_qmlp_s_kernel(
         for half in range(ROW_HALVES):
             window = q_words[:, half * WINDOW_WORDS : (half + 1) * WINDOW_WORDS]
             transposed = transpose_windows(nc, psum_t, identity[:], [window])
-            source = transposed[:, 0, :, :].rearrange("p u r -> p r u")
-            if half % 2 == 0:
-                nc.scalar.copy(out=x_words[:, half, :, :], in_=source)
-            else:
-                nc.vector.tensor_copy(out=x_words[:, half, :, :], in_=source)
+            leave_psum(half, x_words[:, half, :, :], transposed[:, 0, :, :].rearrange("p u r -> p r u"))
         nc.vector.quantize_mx(out=x_codes[:].bitcast(FP8X4), scales=x_scales[:], in_=x_grouped[:])
 
         w1_words = w1_sb[:].bitcast(F32)
@@ -128,11 +134,9 @@ def tile_qmlp_s_kernel(
         for n, c in enumerate(ORDER):
             window = w1_words[:, FIRST_SLOT[c] * WORDS : FIRST_SLOT[c] * WORDS + WINDOW_WORDS]
             transposed = transpose_windows(nc, psum_t, identity[:], [window])
-            source = transposed[:, 0, :, :].rearrange("p u (m t) -> p t m u", t=PACK)
-            if n % 2 == 0:
-                nc.scalar.copy(out=w1_grouped_words[:, :, c, :, :], in_=source)
-            else:
-                nc.vector.tensor_copy(out=w1_grouped_words[:, :, c, :, :], in_=source)
+            leave_psum(
+                n, w1_grouped_words[:, :, c, :, :], transposed[:, 0, :, :].rearrange("p u (m t) -> p t m u", t=PACK)
+            )
         for t in range(PACK):
             cols = slice(t * P, (t + 1) * P)
             nc.vector.quantize_mx(
@@ -141,12 +145,13 @@ def tile_qmlp_s_kernel(
                 in_=w1_grouped[:, t * P * PACK : (t + 1) * P * PACK],
             )
 
-        b2_sb = keep.tile([P, COLUMNS_2], F32)
-        for n in range(COLUMNS_2 // BANK):
-            cols = slice(n * BANK, (n + 1) * BANK)
-            spread = psum_mx.tile([P, BANK], F32, tag="mx")
-            nc.tensor.matmul(out=spread[:], lhsT=ones[:], rhs=b2_rows[:, cols], start=True, stop=True)
-            nc.scalar.copy(out=b2_sb[:, cols], in_=spread[:])
+        fill_signed_slots(
+            nc,
+            w2_slots,
+            lambda out, in_: nc.gpsimd.tensor_scalar(
+                out=out, in0=in_, scalar1=1.0, scalar2=0.0, op0=ALU.mult, op1=ALU.add
+            ),
+        )
 
         h_planes = keep.tile([P, PACK, ROWS], BF16)
         for t in range(PACK):
@@ -168,20 +173,7 @@ def tile_qmlp_s_kernel(
                     out=h_planes[:, t, :], in0=hidden[:], scalar1=b1_sb[:, t : t + 1], scalar2=0.0,
                     op0=ALU.add, op1=ALU.max,
                 )
-        h_grouped = keep.tile([P, ROWS * PACK], BF16, align_bytes=64)
-        h_codes = keep.tile([P, ROWS], U32, align_bytes=64)
-        h_scales = keep.tile([P, ROWS], U8, align_bytes=64)
-        for half in range(ROW_HALVES):
-            rows = slice(half * P, (half + 1) * P)
-            grouped = h_grouped[:, half * P * PACK : (half + 1) * P * PACK]
-            nc.vector.tensor_scalar_mul(
-                out=grouped.rearrange("p (r t) -> p r t", t=PACK),
-                in0=h_planes[:, :, rows].rearrange("p t r -> p r t"),
-                scalar1=sign[:, 0:1],
-            )
-            nc.vector.quantize_mx(out=h_codes[:, rows].bitcast(FP8X4), scales=h_scales[:, rows], in_=grouped)
 
-        fill_signed_slots(nc, w2_slots)
         w2_words = w2_sb[:].bitcast(F32).rearrange("p (t w) -> p t w", t=OUT_TILES)
         windows = [
             w2_words[:, tile, FIRST_SLOT[c] * WORDS : FIRST_SLOT[c] * WORDS + WINDOW_WORDS]
@@ -192,21 +184,31 @@ def tile_qmlp_s_kernel(
         w2_grouped_words = w2_grouped[:].bitcast(F32).rearrange("p (n o u) -> p n o u", o=P, u=2)
         w2_codes = keep.tile([P, COLUMNS_2], U32, align_bytes=64)
         w2_scales = keep.tile([P, COLUMNS_2], U8, align_bytes=64)
+        h_grouped = keep.tile([P, ROWS * PACK], BF16, align_bytes=64)
+        h_codes = keep.tile([P, ROWS], U32, align_bytes=64)
+        h_scales = keep.tile([P, ROWS], U8, align_bytes=64)
+        b2_sb = keep.tile([P, COLUMNS_2], BF16)
         result = keep.tile([P, ROW_HALVES, COLUMNS_2], F32)
-        per_chunk = CHUNK // P
-        for chunk in range(COLUMNS_2 // CHUNK):
-            cols = slice(chunk * CHUNK, (chunk + 1) * CHUNK)
-            first = chunk * per_chunk
-            transposed = transpose_windows(nc, psum_t, identity[:], windows[first : first + per_chunk])
+        products = {}
+
+        def transpose_w2(chunk):
+            first = chunk * (CHUNK // P)
+            last = first + CHUNK // P
+            transposed = transpose_windows(nc, psum_t, identity[:], windows[first:last])
             nc.scalar.copy(
-                out=w2_grouped_words[:, first : first + per_chunk, :, :],
-                in_=transposed[:].rearrange("p n u o -> p n o u"),
+                out=w2_grouped_words[:, first:last, :, :], in_=transposed[:].rearrange("p n u o -> p n o u")
             )
+
+        def quantise_w2(chunk):
+            cols = slice(chunk * CHUNK, (chunk + 1) * CHUNK)
             nc.vector.quantize_mx(
                 out=w2_codes[:, cols].bitcast(FP8X4),
                 scales=w2_scales[:, cols],
                 in_=w2_grouped[:, chunk * CHUNK * PACK : (chunk + 1) * CHUNK * PACK],
             )
+
+        def multiply(chunk):
+            cols = slice(chunk * CHUNK, (chunk + 1) * CHUNK)
             product = psum_mx.tile([P, ROW_HALVES, CHUNK], F32, tag="mx")
             for half in range(ROW_HALVES):
                 rows = slice(half * P, (half + 1) * P)
@@ -219,9 +221,13 @@ def tile_qmlp_s_kernel(
                     start=True,
                     stop=True,
                 )
+            products[chunk] = product
+
+        def add_bias_and_store(chunk):
+            cols = slice(chunk * CHUNK, (chunk + 1) * CHUNK)
             nc.vector.tensor_tensor(
                 out=result[:, :, cols],
-                in0=product[:],
+                in0=products[chunk][:],
                 in1=b2_sb[:, cols].unsqueeze(1).to_broadcast([P, ROW_HALVES, CHUNK]),
                 op=ALU.add,
             )
@@ -231,3 +237,44 @@ def tile_qmlp_s_kernel(
                         out=outs[c].rearrange("(p h) o -> p h o", h=ROW_HALVES),
                         in_=result[:, :, n * D_OUT : (n + 1) * D_OUT],
                     )
+
+        for chunk in range(ROUND):
+            transpose_w2(chunk)
+
+        for first in range(0, COLUMNS_2, 2 * BANK):
+            width = min(2 * BANK, COLUMNS_2 - first)
+            spread = psum_mx.tile([P, width], BF16, tag="mx")
+            for start in range(0, width, BANK):
+                nc.tensor.matmul(
+                    out=spread[:, start : start + BANK],
+                    lhsT=ones[:],
+                    rhs=b2_rows[:, first + start : first + start + BANK],
+                    start=True,
+                    stop=True,
+                )
+            nc.scalar.copy(out=b2_sb[:, first : first + width], in_=spread[:])
+
+        for chunk in range(ROUND, 2 * ROUND):
+            transpose_w2(chunk)
+
+        assert ROW_HALVES == ROUND
+        for half in range(ROW_HALVES):
+            rows = slice(half * P, (half + 1) * P)
+            grouped = h_grouped[:, half * P * PACK : (half + 1) * P * PACK]
+            nc.vector.tensor_scalar_mul(
+                out=grouped.rearrange("p (r t) -> p r t", t=PACK),
+                in0=h_planes[:, :, rows].rearrange("p t r -> p r t"),
+                scalar1=sign[:, 0:1],
+            )
+            quantise_w2(half)
+            nc.vector.quantize_mx(out=h_codes[:, rows].bitcast(FP8X4), scales=h_scales[:, rows], in_=grouped)
+
+        for first in range(0, CHUNKS, ROUND):
+            for chunk in range(first, first + ROUND):
+                multiply(chunk)
+            for chunk in range(first + 2 * ROUND, min(first + 3 * ROUND, CHUNKS)):
+                transpose_w2(chunk)
+            for chunk in range(first, first + ROUND):
+                if chunk + ROUND < CHUNKS:
+                    quantise_w2(chunk + ROUND)
+                add_bias_and_store(chunk)

@@ -26,16 +26,16 @@ COLUMNS_2 = COMPONENTS * D_OUT
 BANK = 512
 CHUNK = 256
 CHUNKS = COLUMNS_2 // CHUNK
-ROUND = 2
+EARLY = 2 * D_OUT // CHUNK
 FLOPS = 2 * ROWS * 512 * (COMPONENTS * FEATURES + COLUMNS_2)
 
 
-def fill_signed_slots(nc, slots, copy):
-    nc.vector.tensor_scalar_mul(out=slots[:, :, 4:6, :], in0=slots[:, :, 0:2, :], scalar1=-1.0)
-    nc.vector.tensor_scalar_mul(out=slots[:, :, 7:11:3, :], in0=slots[:, :, 2:4, :], scalar1=-1.0)
-    copy(slots[:, :, 6, :], slots[:, :, 3, :])
-    copy(slots[:, :, 8:10, :], slots[:, :, 1:5:3, :])
-    copy(slots[:, :, 11, :], slots[:, :, 2, :])
+def fill_signed_slots(slots, second_row, other_rows):
+    second_row(slots[:, :, 4:6, :], slots[:, :, 0:2, :], -1.0)
+    other_rows(slots[:, :, 6, :], slots[:, :, 3, :], 1.0)
+    other_rows(slots[:, :, 7:11:3, :], slots[:, :, 2:4, :], -1.0)
+    other_rows(slots[:, :, 8:10, :], slots[:, :, 1:5:3, :], 1.0)
+    other_rows(slots[:, :, 11, :], slots[:, :, 2, :], 1.0)
 
 
 def transpose_windows(nc, psum, identity, windows):
@@ -92,17 +92,53 @@ def tile_qmlp_s_kernel(
         for c in (I, R, J, K):
             nc.sync.dma_start(out=q_view[:, :, c, :], in_=q[c].rearrange("(p h) f -> p h f", h=ROW_HALVES))
         for c in (J, K, R, I):
-            nc.scalar.dma_start(out=w1_slots[:, 0, RAW_SLOT[c], :], in_=W1[c])
+            nc.scalar.dma_start(
+                out=w2_slots[:, :, RAW_SLOT[c], :], in_=W2[c].rearrange("(t p) f -> p t f", p=P)
+            )
         for n, c in enumerate(ORDER):
             nc.gpsimd.dma_start(out=b2_rows[0:1, n * D_OUT : (n + 1) * D_OUT], in_=b2[c].unsqueeze(0))
         table_warmer = keep.tile([P, 1], F32)
         nc.scalar.activation(out=table_warmer[:], in_=sign[:], func=ACT.Relu)
         for c in (J, K, R, I):
-            nc.sync.dma_start(
-                out=w2_slots[:, :, RAW_SLOT[c], :], in_=W2[c].rearrange("(t p) f -> p t f", p=P)
-            )
+            nc.sync.dma_start(out=w1_slots[:, 0, RAW_SLOT[c], :], in_=W1[c])
         for c in range(COMPONENTS):
-            nc.scalar.dma_start(out=b1_sb[32 * c : 32 * c + 32, :], in_=b1[c].rearrange("(m t) -> m t", t=PACK))
+            nc.sync.dma_start(out=b1_sb[32 * c : 32 * c + 32, :], in_=b1[c].rearrange("(m t) -> m t", t=PACK))
+
+        x_grouped = keep.tile([P, ROWS * PACK], BF16, align_bytes=64)
+        x_codes = keep.tile([P, ROWS], U32, align_bytes=64)
+        x_scales = keep.tile([P, ROWS], U8, align_bytes=64)
+        w1_grouped = keep.tile([P, COMPONENTS * FEATURES * PACK], BF16, align_bytes=64)
+        w1_codes = keep.tile([P, COMPONENTS * FEATURES], U32, align_bytes=64)
+        w1_scales = keep.tile([P, COMPONENTS * FEATURES], U8, align_bytes=64)
+        h_planes = keep.tile([P, PACK, ROWS], BF16)
+        h_grouped = keep.tile([P, ROWS * PACK], BF16, align_bytes=64)
+        h_codes = keep.tile([P, ROWS], U32, align_bytes=64)
+        h_scales = keep.tile([P, ROWS], U8, align_bytes=64)
+        w2_grouped = keep.tile([P, COLUMNS_2 * PACK], BF16, align_bytes=64)
+        w2_codes = keep.tile([P, COLUMNS_2], U32, align_bytes=64)
+        w2_scales = keep.tile([P, COLUMNS_2], U8, align_bytes=64)
+        b2_sb = keep.tile([P, COLUMNS_2], BF16)
+        result = keep.tile([P, ROW_HALVES, COLUMNS_2], F32)
+
+        q_words = q_sb[:].bitcast(F32)
+        x_words = x_grouped[:].bitcast(F32).rearrange("p (h r u) -> p h r u", h=ROW_HALVES, u=2)
+        w1_words = w1_sb[:].bitcast(F32)
+        w1_grouped_words = w1_grouped[:].bitcast(F32).rearrange(
+            "p (t c m u) -> p t c m u", t=PACK, c=COMPONENTS, u=2
+        )
+        w2_words = w2_sb[:].bitcast(F32).rearrange("p (t w) -> p t w", t=OUT_TILES)
+        w2_windows = [
+            w2_words[:, tile, FIRST_SLOT[c] * WORDS : FIRST_SLOT[c] * WORDS + WINDOW_WORDS]
+            for c in ORDER
+            for tile in range(OUT_TILES)
+        ]
+        w2_grouped_words = w2_grouped[:].bitcast(F32).rearrange("p (n o u) -> p n o u", o=P, u=2)
+
+        def on_vector(out, in_, factor):
+            nc.vector.tensor_scalar_mul(out=out, in0=in_, scalar1=factor)
+
+        def on_gpsimd(out, in_, factor):
+            nc.gpsimd.tensor_scalar(out=out, in0=in_, scalar1=factor, scalar2=0.0, op0=ALU.mult, op1=ALU.add)
 
         def leave_psum(piece, out, in_):
             if piece % 2 == 0:
@@ -110,28 +146,37 @@ def tile_qmlp_s_kernel(
             else:
                 nc.scalar.copy(out=out, in_=in_)
 
-        nc.vector.tensor_scalar_mul(out=q_view[:, :, I, :], in0=q_view[:, :, I, :], scalar1=-1.0)
-        fill_signed_slots(nc, w1_slots, lambda out, in_: nc.vector.tensor_copy(out=out, in_=in_))
+        def transpose_w2(chunk):
+            first = chunk * (CHUNK // P)
+            last = first + CHUNK // P
+            transposed = transpose_windows(nc, psum_t, identity[:], w2_windows[first:last])
+            nc.scalar.copy(
+                out=w2_grouped_words[:, first:last, :, :], in_=transposed[:].rearrange("p n u o -> p n o u")
+            )
 
-        q_words = q_sb[:].bitcast(F32)
-        x_grouped = keep.tile([P, ROWS * PACK], BF16, align_bytes=64)
-        x_words = x_grouped[:].bitcast(F32).rearrange("p (h r u) -> p h r u", h=ROW_HALVES, u=2)
-        x_codes = keep.tile([P, ROWS], U32, align_bytes=64)
-        x_scales = keep.tile([P, ROWS], U8, align_bytes=64)
+        def quantise_w2(chunk):
+            cols = slice(chunk * CHUNK, (chunk + 1) * CHUNK)
+            nc.vector.quantize_mx(
+                out=w2_codes[:, cols].bitcast(FP8X4),
+                scales=w2_scales[:, cols],
+                in_=w2_grouped[:, chunk * CHUNK * PACK : (chunk + 1) * CHUNK * PACK],
+            )
+
+        on_vector(q_view[:, :, I, :], q_view[:, :, I, :], -1.0)
         for half in range(ROW_HALVES):
             window = q_words[:, half * WINDOW_WORDS : (half + 1) * WINDOW_WORDS]
             transposed = transpose_windows(nc, psum_t, identity[:], [window])
             leave_psum(half, x_words[:, half, :, :], transposed[:, 0, :, :].rearrange("p u r -> p r u"))
+        fill_signed_slots(w2_slots, on_vector, on_gpsimd)
         nc.vector.quantize_mx(out=x_codes[:].bitcast(FP8X4), scales=x_scales[:], in_=x_grouped[:])
 
-        w1_words = w1_sb[:].bitcast(F32)
-        w1_grouped = keep.tile([P, COMPONENTS * FEATURES * PACK], BF16, align_bytes=64)
-        w1_grouped_words = w1_grouped[:].bitcast(F32).rearrange(
-            "p (t c m u) -> p t c m u", t=PACK, c=COMPONENTS, u=2
-        )
-        w1_codes = keep.tile([P, COMPONENTS * FEATURES], U32, align_bytes=64)
-        w1_scales = keep.tile([P, COMPONENTS * FEATURES], U8, align_bytes=64)
+        for chunk in range(EARLY):
+            transpose_w2(chunk)
+
+        fill_signed_slots(w1_slots, on_vector, on_vector)
         for n, c in enumerate(ORDER):
+            if n < EARLY:
+                quantise_w2(n)
             window = w1_words[:, FIRST_SLOT[c] * WORDS : FIRST_SLOT[c] * WORDS + WINDOW_WORDS]
             transposed = transpose_windows(nc, psum_t, identity[:], [window])
             leave_psum(
@@ -144,16 +189,9 @@ def tile_qmlp_s_kernel(
                 scales=w1_scales[:, cols],
                 in_=w1_grouped[:, t * P * PACK : (t + 1) * P * PACK],
             )
+        transpose_w2(EARLY)
+        quantise_w2(EARLY)
 
-        fill_signed_slots(
-            nc,
-            w2_slots,
-            lambda out, in_: nc.gpsimd.tensor_scalar(
-                out=out, in0=in_, scalar1=1.0, scalar2=0.0, op0=ALU.mult, op1=ALU.add
-            ),
-        )
-
-        h_planes = keep.tile([P, PACK, ROWS], BF16)
         for t in range(PACK):
             cols = slice(t * P, (t + 1) * P)
             hidden = psum_mx.tile([P, ROWS], F32, tag="mx")
@@ -174,40 +212,38 @@ def tile_qmlp_s_kernel(
                     op0=ALU.add, op1=ALU.max,
                 )
 
-        w2_words = w2_sb[:].bitcast(F32).rearrange("p (t w) -> p t w", t=OUT_TILES)
-        windows = [
-            w2_words[:, tile, FIRST_SLOT[c] * WORDS : FIRST_SLOT[c] * WORDS + WINDOW_WORDS]
-            for c in ORDER
-            for tile in range(OUT_TILES)
-        ]
-        w2_grouped = keep.tile([P, COLUMNS_2 * PACK], BF16, align_bytes=64)
-        w2_grouped_words = w2_grouped[:].bitcast(F32).rearrange("p (n o u) -> p n o u", o=P, u=2)
-        w2_codes = keep.tile([P, COLUMNS_2], U32, align_bytes=64)
-        w2_scales = keep.tile([P, COLUMNS_2], U8, align_bytes=64)
-        h_grouped = keep.tile([P, ROWS * PACK], BF16, align_bytes=64)
-        h_codes = keep.tile([P, ROWS], U32, align_bytes=64)
-        h_scales = keep.tile([P, ROWS], U8, align_bytes=64)
-        b2_sb = keep.tile([P, COLUMNS_2], BF16)
-        result = keep.tile([P, ROW_HALVES, COLUMNS_2], F32)
-        products = {}
+        for first in range(0, COLUMNS_2, 2 * BANK):
+            width = min(2 * BANK, COLUMNS_2 - first)
+            spread = psum_mx.tile([P, width], BF16, tag="mx")
+            for start in range(0, width, BANK):
+                nc.tensor.matmul(
+                    out=spread[:, start : start + BANK],
+                    lhsT=ones[:],
+                    rhs=b2_rows[:, first + start : first + start + BANK],
+                    start=True,
+                    stop=True,
+                )
+            nc.scalar.copy(out=b2_sb[:, first : first + width], in_=spread[:])
+        for chunk in range(EARLY + 1, CHUNKS):
+            transpose_w2(chunk)
 
-        def transpose_w2(chunk):
-            first = chunk * (CHUNK // P)
-            last = first + CHUNK // P
-            transposed = transpose_windows(nc, psum_t, identity[:], windows[first:last])
-            nc.scalar.copy(
-                out=w2_grouped_words[:, first:last, :, :], in_=transposed[:].rearrange("p n u o -> p n o u")
+        for half in range(ROW_HALVES):
+            nc.vector.tensor_scalar_mul(
+                out=h_grouped[:, half * P * PACK : (half + 1) * P * PACK].rearrange("p (r t) -> p r t", t=PACK),
+                in0=h_planes[:, :, half * P : (half + 1) * P].rearrange("p t r -> p r t"),
+                scalar1=sign[:, 0:1],
             )
-
-        def quantise_w2(chunk):
-            cols = slice(chunk * CHUNK, (chunk + 1) * CHUNK)
+        for half in range(ROW_HALVES):
+            rows = slice(half * P, (half + 1) * P)
             nc.vector.quantize_mx(
-                out=w2_codes[:, cols].bitcast(FP8X4),
-                scales=w2_scales[:, cols],
-                in_=w2_grouped[:, chunk * CHUNK * PACK : (chunk + 1) * CHUNK * PACK],
+                out=h_codes[:, rows].bitcast(FP8X4),
+                scales=h_scales[:, rows],
+                in_=h_grouped[:, half * P * PACK : (half + 1) * P * PACK],
             )
+        for chunk in range(EARLY + 1, CHUNKS):
+            quantise_w2(chunk)
 
-        def multiply(chunk):
+        for chunk in range(CHUNKS):
             cols = slice(chunk * CHUNK, (chunk + 1) * CHUNK)
             product = psum_mx.tile([P, ROW_HALVES, CHUNK], F32, tag="mx")
             for half in range(ROW_HALVES):
@@ -221,13 +257,9 @@ def tile_qmlp_s_kernel(
                     start=True,
                     stop=True,
                 )
-            products[chunk] = product
-
-        def add_bias_and_store(chunk):
-            cols = slice(chunk * CHUNK, (chunk + 1) * CHUNK)
             nc.vector.tensor_tensor(
                 out=result[:, :, cols],
-                in0=products[chunk][:],
+                in0=product[:],
                 in1=b2_sb[:, cols].unsqueeze(1).to_broadcast([P, ROW_HALVES, CHUNK]),
                 op=ALU.add,
             )
@@ -237,44 +269,3 @@ def tile_qmlp_s_kernel(
                         out=outs[c].rearrange("(p h) o -> p h o", h=ROW_HALVES),
                         in_=result[:, :, n * D_OUT : (n + 1) * D_OUT],
                     )
-
-        for chunk in range(ROUND):
-            transpose_w2(chunk)
-
-        for first in range(0, COLUMNS_2, 2 * BANK):
-            width = min(2 * BANK, COLUMNS_2 - first)
-            spread = psum_mx.tile([P, width], BF16, tag="mx")
-            for start in range(0, width, BANK):
-                nc.tensor.matmul(
-                    out=spread[:, start : start + BANK],
-                    lhsT=ones[:],
-                    rhs=b2_rows[:, first + start : first + start + BANK],
-                    start=True,
-                    stop=True,
-                )
-            nc.scalar.copy(out=b2_sb[:, first : first + width], in_=spread[:])
-
-        for chunk in range(ROUND, 2 * ROUND):
-            transpose_w2(chunk)
-
-        assert ROW_HALVES == ROUND
-        for half in range(ROW_HALVES):
-            rows = slice(half * P, (half + 1) * P)
-            grouped = h_grouped[:, half * P * PACK : (half + 1) * P * PACK]
-            nc.vector.tensor_scalar_mul(
-                out=grouped.rearrange("p (r t) -> p r t", t=PACK),
-                in0=h_planes[:, :, rows].rearrange("p t r -> p r t"),
-                scalar1=sign[:, 0:1],
-            )
-            quantise_w2(half)
-            nc.vector.quantize_mx(out=h_codes[:, rows].bitcast(FP8X4), scales=h_scales[:, rows], in_=grouped)
-
-        for first in range(0, CHUNKS, ROUND):
-            for chunk in range(first, first + ROUND):
-                multiply(chunk)
-            for chunk in range(first + 2 * ROUND, min(first + 3 * ROUND, CHUNKS)):
-                transpose_w2(chunk)
-            for chunk in range(first, first + ROUND):
-                if chunk + ROUND < CHUNKS:
-                    quantise_w2(chunk + ROUND)
-                add_bias_and_store(chunk)

@@ -16,9 +16,9 @@ ROWS, FEATURES, D_OUT = 256, 128, 384
 ROW_HALVES = ROWS // P
 WORDS = FEATURES // 2
 WINDOW_WORDS = COMPONENTS * WORDS
-SLOTS = 12
+SLOTS = 6
 R, I, J, K = 0, 1, 2, 3
-FIRST_SLOT = {J: 0, R: 2, I: 6, K: 8}
+WINDOW = {J: (0, 0), R: (0, 2), I: (1, 0), K: (1, 2)}
 RAW_SLOT = {J: 0, K: 1, R: 2, I: 3}
 ORDER = (J, R, I, K)
 OUT_TILES = D_OUT // P
@@ -27,15 +27,16 @@ BANK = 512
 CHUNK = 256
 CHUNKS = COLUMNS_2 // CHUNK
 EARLY = 2 * D_OUT // CHUNK
+LEAD = 2
 FLOPS = 2 * ROWS * 512 * (COMPONENTS * FEATURES + COLUMNS_2)
 
 
-def fill_signed_slots(slots, second_row, other_rows):
-    second_row(slots[:, :, 4:6, :], slots[:, :, 0:2, :], -1.0)
-    other_rows(slots[:, :, 6, :], slots[:, :, 3, :], 1.0)
-    other_rows(slots[:, :, 7:11:3, :], slots[:, :, 2:4, :], -1.0)
-    other_rows(slots[:, :, 8:10, :], slots[:, :, 1:5:3, :], 1.0)
-    other_rows(slots[:, :, 11, :], slots[:, :, 2, :], 1.0)
+def fill_signed_slots(nc, first, second, copy):
+    nc.vector.tensor_scalar_mul(out=first[:, :, 4:6, :], in0=first[:, :, 0:2, :], scalar1=-1.0)
+    nc.vector.tensor_scalar_mul(out=second[:, :, 1:5:3, :], in0=first[:, :, 2:4, :], scalar1=-1.0)
+    copy(second[:, :, 0, :], first[:, :, 3, :])
+    copy(second[:, :, 2:4, :], first[:, :, 1:5:3, :])
+    copy(second[:, :, 5, :], first[:, :, 2, :])
 
 
 def transpose_windows(nc, psum, identity, windows):
@@ -83,62 +84,28 @@ def tile_qmlp_s_kernel(
 
         q_sb = keep.tile([P, ROW_HALVES * COMPONENTS * FEATURES], BF16)
         q_view = q_sb[:].rearrange("p (h c f) -> p h c f", h=ROW_HALVES, c=COMPONENTS)
-        w1_sb = keep.tile([P, SLOTS * FEATURES], BF16)
-        w1_slots = w1_sb[:].rearrange("p (t s f) -> p t s f", t=1, s=SLOTS)
-        w2_sb = keep.tile([P, OUT_TILES * SLOTS * FEATURES], BF16)
-        w2_slots = w2_sb[:].rearrange("p (t s f) -> p t s f", t=OUT_TILES, s=SLOTS)
+        w1_first = keep.tile([P, SLOTS * FEATURES], BF16)
+        w1_second = keep.tile([P, SLOTS * FEATURES], BF16)
+        w1_slots = [a[:].rearrange("p (t s f) -> p t s f", t=1, s=SLOTS) for a in (w1_first, w1_second)]
+        w2_first = keep.tile([P, OUT_TILES * SLOTS * FEATURES], BF16)
+        w2_second = keep.tile([P, OUT_TILES * SLOTS * FEATURES], BF16)
+        w2_slots = [a[:].rearrange("p (t s f) -> p t s f", t=OUT_TILES, s=SLOTS) for a in (w2_first, w2_second)]
         b1_sb = keep.tile([P, PACK], BF16)
 
         for c in (I, R, J, K):
             nc.sync.dma_start(out=q_view[:, :, c, :], in_=q[c].rearrange("(p h) f -> p h f", h=ROW_HALVES))
         for c in (J, K, R, I):
-            nc.scalar.dma_start(
-                out=w2_slots[:, :, RAW_SLOT[c], :], in_=W2[c].rearrange("(t p) f -> p t f", p=P)
-            )
+            nc.scalar.dma_start(out=w1_slots[0][:, 0, RAW_SLOT[c], :], in_=W1[c])
         for n, c in enumerate(ORDER):
             nc.gpsimd.dma_start(out=b2_rows[0:1, n * D_OUT : (n + 1) * D_OUT], in_=b2[c].unsqueeze(0))
         table_warmer = keep.tile([P, 1], F32)
         nc.scalar.activation(out=table_warmer[:], in_=sign[:], func=ACT.Relu)
         for c in (J, K, R, I):
-            nc.sync.dma_start(out=w1_slots[:, 0, RAW_SLOT[c], :], in_=W1[c])
+            nc.sync.dma_start(
+                out=w2_slots[0][:, :, RAW_SLOT[c], :], in_=W2[c].rearrange("(t p) f -> p t f", p=P)
+            )
         for c in range(COMPONENTS):
-            nc.sync.dma_start(out=b1_sb[32 * c : 32 * c + 32, :], in_=b1[c].rearrange("(m t) -> m t", t=PACK))
-
-        x_grouped = keep.tile([P, ROWS * PACK], BF16, align_bytes=64)
-        x_codes = keep.tile([P, ROWS], U32, align_bytes=64)
-        x_scales = keep.tile([P, ROWS], U8, align_bytes=64)
-        w1_grouped = keep.tile([P, COMPONENTS * FEATURES * PACK], BF16, align_bytes=64)
-        w1_codes = keep.tile([P, COMPONENTS * FEATURES], U32, align_bytes=64)
-        w1_scales = keep.tile([P, COMPONENTS * FEATURES], U8, align_bytes=64)
-        h_planes = keep.tile([P, PACK, ROWS], BF16)
-        h_grouped = keep.tile([P, ROWS * PACK], BF16, align_bytes=64)
-        h_codes = keep.tile([P, ROWS], U32, align_bytes=64)
-        h_scales = keep.tile([P, ROWS], U8, align_bytes=64)
-        w2_grouped = keep.tile([P, COLUMNS_2 * PACK], BF16, align_bytes=64)
-        w2_codes = keep.tile([P, COLUMNS_2], U32, align_bytes=64)
-        w2_scales = keep.tile([P, COLUMNS_2], U8, align_bytes=64)
-        b2_sb = keep.tile([P, COLUMNS_2], BF16)
-        result = keep.tile([P, ROW_HALVES, COLUMNS_2], F32)
-
-        q_words = q_sb[:].bitcast(F32)
-        x_words = x_grouped[:].bitcast(F32).rearrange("p (h r u) -> p h r u", h=ROW_HALVES, u=2)
-        w1_words = w1_sb[:].bitcast(F32)
-        w1_grouped_words = w1_grouped[:].bitcast(F32).rearrange(
-            "p (t c m u) -> p t c m u", t=PACK, c=COMPONENTS, u=2
-        )
-        w2_words = w2_sb[:].bitcast(F32).rearrange("p (t w) -> p t w", t=OUT_TILES)
-        w2_windows = [
-            w2_words[:, tile, FIRST_SLOT[c] * WORDS : FIRST_SLOT[c] * WORDS + WINDOW_WORDS]
-            for c in ORDER
-            for tile in range(OUT_TILES)
-        ]
-        w2_grouped_words = w2_grouped[:].bitcast(F32).rearrange("p (n o u) -> p n o u", o=P, u=2)
-
-        def on_vector(out, in_, factor):
-            nc.vector.tensor_scalar_mul(out=out, in0=in_, scalar1=factor)
-
-        def on_gpsimd(out, in_, factor):
-            nc.gpsimd.tensor_scalar(out=out, in0=in_, scalar1=factor, scalar2=0.0, op0=ALU.mult, op1=ALU.add)
+            nc.scalar.dma_start(out=b1_sb[32 * c : 32 * c + 32, :], in_=b1[c].rearrange("(m t) -> m t", t=PACK))
 
         def leave_psum(piece, out, in_):
             if piece % 2 == 0:
@@ -146,38 +113,30 @@ def tile_qmlp_s_kernel(
             else:
                 nc.scalar.copy(out=out, in_=in_)
 
-        def transpose_w2(chunk):
-            first = chunk * (CHUNK // P)
-            last = first + CHUNK // P
-            transposed = transpose_windows(nc, psum_t, identity[:], w2_windows[first:last])
-            nc.scalar.copy(
-                out=w2_grouped_words[:, first:last, :, :], in_=transposed[:].rearrange("p n u o -> p n o u")
-            )
+        nc.vector.tensor_scalar_mul(out=q_view[:, :, I, :], in0=q_view[:, :, I, :], scalar1=-1.0)
+        fill_signed_slots(nc, w1_slots[0], w1_slots[1], lambda out, in_: nc.vector.tensor_copy(out=out, in_=in_))
 
-        def quantise_w2(chunk):
-            cols = slice(chunk * CHUNK, (chunk + 1) * CHUNK)
-            nc.vector.quantize_mx(
-                out=w2_codes[:, cols].bitcast(FP8X4),
-                scales=w2_scales[:, cols],
-                in_=w2_grouped[:, chunk * CHUNK * PACK : (chunk + 1) * CHUNK * PACK],
-            )
-
-        on_vector(q_view[:, :, I, :], q_view[:, :, I, :], -1.0)
+        q_words = q_sb[:].bitcast(F32)
+        x_grouped = keep.tile([P, ROWS * PACK], BF16, align_bytes=64)
+        x_words = x_grouped[:].bitcast(F32).rearrange("p (h r u) -> p h r u", h=ROW_HALVES, u=2)
+        x_codes = keep.tile([P, ROWS], U32, align_bytes=64)
+        x_scales = keep.tile([P, ROWS], U8, align_bytes=64)
         for half in range(ROW_HALVES):
             window = q_words[:, half * WINDOW_WORDS : (half + 1) * WINDOW_WORDS]
             transposed = transpose_windows(nc, psum_t, identity[:], [window])
             leave_psum(half, x_words[:, half, :, :], transposed[:, 0, :, :].rearrange("p u r -> p r u"))
-        fill_signed_slots(w2_slots, on_vector, on_gpsimd)
         nc.vector.quantize_mx(out=x_codes[:].bitcast(FP8X4), scales=x_scales[:], in_=x_grouped[:])
 
-        for chunk in range(EARLY):
-            transpose_w2(chunk)
-
-        fill_signed_slots(w1_slots, on_vector, on_vector)
+        w1_words = [a[:].bitcast(F32) for a in (w1_first, w1_second)]
+        w1_grouped = keep.tile([P, COMPONENTS * FEATURES * PACK], BF16, align_bytes=64)
+        w1_grouped_words = w1_grouped[:].bitcast(F32).rearrange(
+            "p (t c m u) -> p t c m u", t=PACK, c=COMPONENTS, u=2
+        )
+        w1_codes = keep.tile([P, COMPONENTS * FEATURES], U32, align_bytes=64)
+        w1_scales = keep.tile([P, COMPONENTS * FEATURES], U8, align_bytes=64)
         for n, c in enumerate(ORDER):
-            if n < EARLY:
-                quantise_w2(n)
-            window = w1_words[:, FIRST_SLOT[c] * WORDS : FIRST_SLOT[c] * WORDS + WINDOW_WORDS]
+            array, slot = WINDOW[c]
+            window = w1_words[array][:, slot * WORDS : slot * WORDS + WINDOW_WORDS]
             transposed = transpose_windows(nc, psum_t, identity[:], [window])
             leave_psum(
                 n, w1_grouped_words[:, :, c, :, :], transposed[:, 0, :, :].rearrange("p u (m t) -> p t m u", t=PACK)
@@ -189,9 +148,17 @@ def tile_qmlp_s_kernel(
                 scales=w1_scales[:, cols],
                 in_=w1_grouped[:, t * P * PACK : (t + 1) * P * PACK],
             )
-        transpose_w2(EARLY)
-        quantise_w2(EARLY)
 
+        fill_signed_slots(
+            nc,
+            w2_slots[0],
+            w2_slots[1],
+            lambda out, in_: nc.gpsimd.tensor_scalar(
+                out=out, in0=in_, scalar1=1.0, scalar2=0.0, op0=ALU.mult, op1=ALU.add
+            ),
+        )
+
+        h_planes = keep.tile([P, PACK, ROWS], BF16)
         for t in range(PACK):
             cols = slice(t * P, (t + 1) * P)
             hidden = psum_mx.tile([P, ROWS], F32, tag="mx")
@@ -212,38 +179,40 @@ def tile_qmlp_s_kernel(
                     op0=ALU.add, op1=ALU.max,
                 )
 
-        for first in range(0, COLUMNS_2, 2 * BANK):
-            width = min(2 * BANK, COLUMNS_2 - first)
-            spread = psum_mx.tile([P, width], BF16, tag="mx")
-            for start in range(0, width, BANK):
-                nc.tensor.matmul(
-                    out=spread[:, start : start + BANK],
-                    lhsT=ones[:],
-                    rhs=b2_rows[:, first + start : first + start + BANK],
-                    start=True,
-                    stop=True,
-                )
-            nc.scalar.copy(out=b2_sb[:, first : first + width], in_=spread[:])
-        for chunk in range(EARLY + 1, CHUNKS):
-            transpose_w2(chunk)
+        w2_words = [a[:].bitcast(F32).rearrange("p (t w) -> p t w", t=OUT_TILES) for a in (w2_first, w2_second)]
+        windows = [
+            w2_words[WINDOW[c][0]][:, tile, WINDOW[c][1] * WORDS : WINDOW[c][1] * WORDS + WINDOW_WORDS]
+            for c in ORDER
+            for tile in range(OUT_TILES)
+        ]
+        w2_grouped = keep.tile([P, COLUMNS_2 * PACK], BF16, align_bytes=64)
+        w2_grouped_words = w2_grouped[:].bitcast(F32).rearrange("p (n o u) -> p n o u", o=P, u=2)
+        w2_codes = keep.tile([P, COLUMNS_2], U32, align_bytes=64)
+        w2_scales = keep.tile([P, COLUMNS_2], U8, align_bytes=64)
+        h_grouped = keep.tile([P, ROWS * PACK], BF16, align_bytes=64)
+        h_codes = keep.tile([P, ROWS], U32, align_bytes=64)
+        h_scales = keep.tile([P, ROWS], U8, align_bytes=64)
+        b2_sb = keep.tile([P, COLUMNS_2], BF16)
+        result = keep.tile([P, CHUNKS, ROW_HALVES, CHUNK], F32)
+        products = {}
 
-        for half in range(ROW_HALVES):
-            nc.vector.tensor_scalar_mul(
-                out=h_grouped[:, half * P * PACK : (half + 1) * P * PACK].rearrange("p (r t) -> p r t", t=PACK),
-                in0=h_planes[:, :, half * P : (half + 1) * P].rearrange("p t r -> p r t"),
-                scalar1=sign[:, 0:1],
+        def transpose_w2(chunk):
+            first = chunk * (CHUNK // P)
+            last = first + CHUNK // P
+            transposed = transpose_windows(nc, psum_t, identity[:], windows[first:last])
+            nc.scalar.copy(
+                out=w2_grouped_words[:, first:last, :, :], in_=transposed[:].rearrange("p n u o -> p n o u")
             )
-        for half in range(ROW_HALVES):
-            rows = slice(half * P, (half + 1) * P)
+
+        def quantise_w2(chunk):
+            cols = slice(chunk * CHUNK, (chunk + 1) * CHUNK)
             nc.vector.quantize_mx(
-                out=h_codes[:, rows].bitcast(FP8X4),
-                scales=h_scales[:, rows],
-                in_=h_grouped[:, half * P * PACK : (half + 1) * P * PACK],
+                out=w2_codes[:, cols].bitcast(FP8X4),
+                scales=w2_scales[:, cols],
+                in_=w2_grouped[:, chunk * CHUNK * PACK : (chunk + 1) * CHUNK * PACK],
             )
-        for chunk in range(EARLY + 1, CHUNKS):
-            quantise_w2(chunk)
 
-        for chunk in range(CHUNKS):
+        def multiply(chunk):
             cols = slice(chunk * CHUNK, (chunk + 1) * CHUNK)
             product = psum_mx.tile([P, ROW_HALVES, CHUNK], F32, tag="mx")
             for half in range(ROW_HALVES):
@@ -257,15 +226,63 @@ def tile_qmlp_s_kernel(
                     start=True,
                     stop=True,
                 )
+            products[chunk] = product
+
+        def add_bias_and_store(chunk):
+            cols = slice(chunk * CHUNK, (chunk + 1) * CHUNK)
             nc.vector.tensor_tensor(
-                out=result[:, :, cols],
-                in0=product[:],
+                out=result[:, chunk, :, :],
+                in0=products[chunk][:],
                 in1=b2_sb[:, cols].unsqueeze(1).to_broadcast([P, ROW_HALVES, CHUNK]),
                 op=ALU.add,
             )
             for n, c in enumerate(ORDER):
-                if ((n + 1) * D_OUT - 1) // CHUNK == chunk:
+                low = max(chunk * CHUNK, n * D_OUT)
+                high = min((chunk + 1) * CHUNK, (n + 1) * D_OUT)
+                if low < high:
                     nc.sync.dma_start(
-                        out=outs[c].rearrange("(p h) o -> p h o", h=ROW_HALVES),
-                        in_=result[:, :, n * D_OUT : (n + 1) * D_OUT],
+                        out=outs[c].rearrange("(p h) o -> p h o", h=ROW_HALVES)[:, :, low - n * D_OUT : high - n * D_OUT],
+                        in_=result[:, chunk, :, low - chunk * CHUNK : high - chunk * CHUNK],
                     )
+
+        for chunk in range(EARLY):
+            transpose_w2(chunk)
+
+        for first in range(0, COLUMNS_2, 2 * BANK):
+            width = min(2 * BANK, COLUMNS_2 - first)
+            spread = psum_mx.tile([P, width], BF16, tag="mx")
+            for start in range(0, width, BANK):
+                nc.tensor.matmul(
+                    out=spread[:, start : start + BANK],
+                    lhsT=ones[:],
+                    rhs=b2_rows[:, first + start : first + start + BANK],
+                    start=True,
+                    stop=True,
+                )
+            nc.scalar.copy(out=b2_sb[:, first : first + width], in_=spread[:])
+
+        transpose_w2(EARLY)
+
+        for half in range(ROW_HALVES):
+            rows = slice(half * P, (half + 1) * P)
+            grouped = h_grouped[:, half * P * PACK : (half + 1) * P * PACK]
+            nc.vector.tensor_scalar_mul(
+                out=grouped.rearrange("p (r t) -> p r t", t=PACK),
+                in0=h_planes[:, :, rows].rearrange("p t r -> p r t"),
+                scalar1=sign[:, 0:1],
+            )
+            quantise_w2(half)
+            nc.vector.quantize_mx(out=h_codes[:, rows].bitcast(FP8X4), scales=h_scales[:, rows], in_=grouped)
+        for chunk in range(ROW_HALVES, EARLY):
+            quantise_w2(chunk)
+
+        for chunk in range(EARLY):
+            multiply(chunk)
+        for chunk in range(EARLY + 1, CHUNKS):
+            transpose_w2(chunk)
+        for chunk in range(CHUNKS):
+            if chunk >= EARLY:
+                multiply(chunk)
+            add_bias_and_store(chunk)
+            if EARLY <= chunk + LEAD < CHUNKS:
+                quantise_w2(chunk + LEAD)

@@ -31,8 +31,11 @@ LEAD = 2
 FLOPS = 2 * ROWS * 512 * (COMPONENTS * FEATURES + COLUMNS_2)
 
 
-def fill_signed_slots(nc, first, second, copy):
+def complete_first_array(nc, first):
     nc.vector.tensor_scalar_mul(out=first[:, :, 4:6, :], in0=first[:, :, 0:2, :], scalar1=-1.0)
+
+
+def fill_second_array(nc, first, second, copy):
     nc.vector.tensor_scalar_mul(out=second[:, :, 1:5:3, :], in0=first[:, :, 2:4, :], scalar1=-1.0)
     copy(second[:, :, 0, :], first[:, :, 3, :])
     copy(second[:, :, 2:4, :], first[:, :, 1:5:3, :])
@@ -92,10 +95,13 @@ def tile_qmlp_s_kernel(
         w2_slots = [a[:].rearrange("p (t s f) -> p t s f", t=OUT_TILES, s=SLOTS) for a in (w2_first, w2_second)]
         b1_sb = keep.tile([P, PACK], BF16)
 
-        for c in (I, R, J, K):
-            nc.sync.dma_start(out=q_view[:, :, c, :], in_=q[c].rearrange("(p h) f -> p h f", h=ROW_HALVES))
-        for c in (J, K, R, I):
-            nc.scalar.dma_start(out=w1_slots[0][:, 0, RAW_SLOT[c], :], in_=W1[c])
+        hardware_queues = (nc.sync, nc.scalar)
+        for n, c in enumerate((J, K, R, I)):
+            hardware_queues[n % 2].dma_start(out=w1_slots[0][:, 0, RAW_SLOT[c], :], in_=W1[c])
+        for n, c in enumerate((I, R, J, K)):
+            hardware_queues[n % 2].dma_start(
+                out=q_view[:, :, c, :], in_=q[c].rearrange("(p h) f -> p h f", h=ROW_HALVES)
+            )
         for n, c in enumerate(ORDER):
             nc.gpsimd.dma_start(out=b2_rows[0:1, n * D_OUT : (n + 1) * D_OUT], in_=b2[c].unsqueeze(0))
         table_warmer = keep.tile([P, 1], F32)
@@ -105,7 +111,7 @@ def tile_qmlp_s_kernel(
                 out=w2_slots[0][:, :, RAW_SLOT[c], :], in_=W2[c].rearrange("(t p) f -> p t f", p=P)
             )
         for c in range(COMPONENTS):
-            nc.scalar.dma_start(out=b1_sb[32 * c : 32 * c + 32, :], in_=b1[c].rearrange("(m t) -> m t", t=PACK))
+            nc.sync.dma_start(out=b1_sb[32 * c : 32 * c + 32, :], in_=b1[c].rearrange("(m t) -> m t", t=PACK))
 
         def leave_psum(piece, out, in_):
             if piece % 2 == 0:
@@ -113,20 +119,9 @@ def tile_qmlp_s_kernel(
             else:
                 nc.scalar.copy(out=out, in_=in_)
 
+        complete_first_array(nc, w1_slots[0])
+        fill_second_array(nc, w1_slots[0], w1_slots[1], lambda out, in_: nc.vector.tensor_copy(out=out, in_=in_))
         nc.vector.tensor_scalar_mul(out=q_view[:, :, I, :], in0=q_view[:, :, I, :], scalar1=-1.0)
-        fill_signed_slots(nc, w1_slots[0], w1_slots[1], lambda out, in_: nc.vector.tensor_copy(out=out, in_=in_))
-
-        q_words = q_sb[:].bitcast(F32)
-        x_grouped = keep.tile([P, ROWS * PACK], BF16, align_bytes=64)
-        x_words = x_grouped[:].bitcast(F32).rearrange("p (h r u) -> p h r u", h=ROW_HALVES, u=2)
-        x_codes = keep.tile([P, ROWS], U32, align_bytes=64)
-        x_scales = keep.tile([P, ROWS], U8, align_bytes=64)
-        for half in range(ROW_HALVES):
-            window = q_words[:, half * WINDOW_WORDS : (half + 1) * WINDOW_WORDS]
-            transposed = transpose_windows(nc, psum_t, identity[:], [window])
-            leave_psum(half, x_words[:, half, :, :], transposed[:, 0, :, :].rearrange("p u r -> p r u"))
-        nc.vector.quantize_mx(out=x_codes[:].bitcast(FP8X4), scales=x_scales[:], in_=x_grouped[:])
-
         w1_words = [a[:].bitcast(F32) for a in (w1_first, w1_second)]
         w1_grouped = keep.tile([P, COMPONENTS * FEATURES * PACK], BF16, align_bytes=64)
         w1_grouped_words = w1_grouped[:].bitcast(F32).rearrange(
@@ -141,6 +136,16 @@ def tile_qmlp_s_kernel(
             leave_psum(
                 n, w1_grouped_words[:, :, c, :, :], transposed[:, 0, :, :].rearrange("p u (m t) -> p t m u", t=PACK)
             )
+
+        q_words = q_sb[:].bitcast(F32)
+        x_grouped = keep.tile([P, ROWS * PACK], BF16, align_bytes=64)
+        x_words = x_grouped[:].bitcast(F32).rearrange("p (h r u) -> p h r u", h=ROW_HALVES, u=2)
+        x_codes = keep.tile([P, ROWS], U32, align_bytes=64)
+        x_scales = keep.tile([P, ROWS], U8, align_bytes=64)
+        for half in range(ROW_HALVES):
+            window = q_words[:, half * WINDOW_WORDS : (half + 1) * WINDOW_WORDS]
+            transposed = transpose_windows(nc, psum_t, identity[:], [window])
+            leave_psum(half, x_words[:, half, :, :], transposed[:, 0, :, :].rearrange("p u r -> p r u"))
         for t in range(PACK):
             cols = slice(t * P, (t + 1) * P)
             nc.vector.quantize_mx(
@@ -148,15 +153,9 @@ def tile_qmlp_s_kernel(
                 scales=w1_scales[:, cols],
                 in_=w1_grouped[:, t * P * PACK : (t + 1) * P * PACK],
             )
+        nc.vector.quantize_mx(out=x_codes[:].bitcast(FP8X4), scales=x_scales[:], in_=x_grouped[:])
 
-        fill_signed_slots(
-            nc,
-            w2_slots[0],
-            w2_slots[1],
-            lambda out, in_: nc.gpsimd.tensor_scalar(
-                out=out, in0=in_, scalar1=1.0, scalar2=0.0, op0=ALU.mult, op1=ALU.add
-            ),
-        )
+        complete_first_array(nc, w2_slots[0])
 
         h_planes = keep.tile([P, PACK, ROWS], BF16)
         for t in range(PACK):
@@ -261,19 +260,30 @@ def tile_qmlp_s_kernel(
                 )
             nc.scalar.copy(out=b2_sb[:, first : first + width], in_=spread[:])
 
-        transpose_w2(EARLY)
-
         for half in range(ROW_HALVES):
-            rows = slice(half * P, (half + 1) * P)
-            grouped = h_grouped[:, half * P * PACK : (half + 1) * P * PACK]
             nc.vector.tensor_scalar_mul(
-                out=grouped.rearrange("p (r t) -> p r t", t=PACK),
-                in0=h_planes[:, :, rows].rearrange("p t r -> p r t"),
+                out=h_grouped[:, half * P * PACK : (half + 1) * P * PACK].rearrange("p (r t) -> p r t", t=PACK),
+                in0=h_planes[:, :, half * P : (half + 1) * P].rearrange("p t r -> p r t"),
                 scalar1=sign[:, 0:1],
             )
-            quantise_w2(half)
-            nc.vector.quantize_mx(out=h_codes[:, rows].bitcast(FP8X4), scales=h_scales[:, rows], in_=grouped)
-        for chunk in range(ROW_HALVES, EARLY):
+        for half in range(ROW_HALVES):
+            rows = slice(half * P, (half + 1) * P)
+            nc.vector.quantize_mx(
+                out=h_codes[:, rows].bitcast(FP8X4),
+                scales=h_scales[:, rows],
+                in_=h_grouped[:, half * P * PACK : (half + 1) * P * PACK],
+            )
+
+        fill_second_array(
+            nc,
+            w2_slots[0],
+            w2_slots[1],
+            lambda out, in_: nc.gpsimd.tensor_scalar(
+                out=out, in0=in_, scalar1=1.0, scalar2=0.0, op0=ALU.mult, op1=ALU.add
+            ),
+        )
+        transpose_w2(EARLY)
+        for chunk in range(EARLY):
             quantise_w2(chunk)
 
         for chunk in range(EARLY):

@@ -112,6 +112,10 @@ def tile_qmlp_s_kernel(
             )
         for c in range(COMPONENTS):
             nc.sync.dma_start(out=b1_sb[32 * c : 32 * c + 32, :], in_=b1[c].rearrange("(m t) -> m t", t=PACK))
+        for c, slot in ((I, 0), (K, 2), (R, 5)):
+            nc.sync.dma_start(
+                out=w2_slots[1][:, :, slot, :], in_=W2[c].rearrange("(t p) f -> p t f", p=P)
+            )
 
         def leave_psum(piece, out, in_):
             if piece % 2 == 0:
@@ -274,14 +278,10 @@ def tile_qmlp_s_kernel(
                 in_=h_grouped[:, half * P * PACK : (half + 1) * P * PACK],
             )
 
-        fill_second_array(
-            nc,
-            w2_slots[0],
-            w2_slots[1],
-            lambda out, in_: nc.gpsimd.tensor_scalar(
-                out=out, in0=in_, scalar1=1.0, scalar2=0.0, op0=ALU.mult, op1=ALU.add
-            ),
+        nc.vector.tensor_scalar_mul(
+            out=w2_slots[1][:, :, 1:5:3, :], in0=w2_slots[0][:, :, 2:4, :], scalar1=-1.0
         )
+        nc.vector.tensor_scalar_mul(out=w2_slots[1][:, :, 3, :], in0=w2_slots[0][:, :, 0, :], scalar1=-1.0)
         transpose_w2(EARLY)
         for chunk in range(EARLY):
             quantise_w2(chunk)

@@ -102,8 +102,6 @@ def tile_qmlp_s_kernel(
             hardware_queues[n % 2].dma_start(
                 out=q_view[:, :, c, :], in_=q[c].rearrange("(p h) f -> p h f", h=ROW_HALVES)
             )
-        for n, c in enumerate(ORDER):
-            nc.gpsimd.dma_start(out=b2_rows[0:1, n * D_OUT : (n + 1) * D_OUT], in_=b2[c].unsqueeze(0))
         table_warmer = keep.tile([P, 1], F32)
         nc.scalar.activation(out=table_warmer[:], in_=sign[:], func=ACT.Relu)
         for c in (J, K, R, I):
@@ -112,6 +110,8 @@ def tile_qmlp_s_kernel(
             )
         for c in range(COMPONENTS):
             nc.sync.dma_start(out=b1_sb[32 * c : 32 * c + 32, :], in_=b1[c].rearrange("(m t) -> m t", t=PACK))
+        for n, c in enumerate(ORDER):
+            nc.sync.dma_start(out=b2_rows[0:1, n * D_OUT : (n + 1) * D_OUT], in_=b2[c].unsqueeze(0))
         for c, slot in ((I, 0), (K, 2), (R, 5)):
             nc.sync.dma_start(
                 out=w2_slots[1][:, :, slot, :], in_=W2[c].rearrange("(t p) f -> p t f", p=P)

@@ -27,19 +27,7 @@ BANK = 512
 CHUNK = 256
 CHUNKS = COLUMNS_2 // CHUNK
 EARLY = 2 * D_OUT // CHUNK
-LEAD = 2
 FLOPS = 2 * ROWS * 512 * (COMPONENTS * FEATURES + COLUMNS_2)
-
-
-def complete_first_array(nc, first):
-    nc.vector.tensor_scalar_mul(out=first[:, :, 4:6, :], in0=first[:, :, 0:2, :], scalar1=-1.0)
-
-
-def fill_second_array(nc, first, second, copy):
-    nc.vector.tensor_scalar_mul(out=second[:, :, 1:5:3, :], in0=first[:, :, 2:4, :], scalar1=-1.0)
-    copy(second[:, :, 0, :], first[:, :, 3, :])
-    copy(second[:, :, 2:4, :], first[:, :, 1:5:3, :])
-    copy(second[:, :, 5, :], first[:, :, 2, :])
 
 
 def transpose_windows(nc, psum, identity, windows):
@@ -112,20 +100,16 @@ def tile_qmlp_s_kernel(
             nc.sync.dma_start(out=b1_sb[32 * c : 32 * c + 32, :], in_=b1[c].rearrange("(m t) -> m t", t=PACK))
         for n, c in enumerate(ORDER):
             nc.sync.dma_start(out=b2_rows[0:1, n * D_OUT : (n + 1) * D_OUT], in_=b2[c].unsqueeze(0))
-        for c, slot in ((I, 0), (K, 2), (R, 5)):
-            nc.sync.dma_start(
-                out=w2_slots[1][:, :, slot, :], in_=W2[c].rearrange("(t p) f -> p t f", p=P)
-            )
 
-        def leave_psum(piece, out, in_):
-            if piece % 2 == 0:
+        def leave_psum(engine, out, in_):
+            if engine == "V":
                 nc.vector.tensor_copy(out=out, in_=in_)
             else:
                 nc.scalar.copy(out=out, in_=in_)
 
-        complete_first_array(nc, w1_slots[0])
-        fill_second_array(nc, w1_slots[0], w1_slots[1], lambda out, in_: nc.vector.tensor_copy(out=out, in_=in_))
-        nc.vector.tensor_scalar_mul(out=q_view[:, :, I, :], in0=q_view[:, :, I, :], scalar1=-1.0)
+        def negate(out, in_):
+            nc.vector.tensor_scalar_mul(out=out, in0=in_, scalar1=-1.0)
+
         w1_words = [a[:].bitcast(F32) for a in (w1_first, w1_second)]
         w1_grouped = keep.tile([P, COMPONENTS * FEATURES * PACK], BF16, align_bytes=64)
         w1_grouped_words = w1_grouped[:].bitcast(F32).rearrange(
@@ -133,12 +117,18 @@ def tile_qmlp_s_kernel(
         )
         w1_codes = keep.tile([P, COMPONENTS * FEATURES], U32, align_bytes=64)
         w1_scales = keep.tile([P, COMPONENTS * FEATURES], U8, align_bytes=64)
-        for n, c in enumerate(ORDER):
-            array, slot = WINDOW[c]
+        w1_t = {}
+
+        def transpose_w1(n):
+            array, slot = WINDOW[ORDER[n]]
             window = w1_words[array][:, slot * WORDS : slot * WORDS + WINDOW_WORDS]
-            transposed = transpose_windows(nc, psum_t, identity[:], [window])
+            w1_t[n] = transpose_windows(nc, psum_t, identity[:], [window])
+
+        def leave_w1(n, engine):
             leave_psum(
-                n, w1_grouped_words[:, :, c, :, :], transposed[:, 0, :, :].rearrange("p u (m t) -> p t m u", t=PACK)
+                engine,
+                w1_grouped_words[:, :, ORDER[n], :, :],
+                w1_t[n][:, 0, :, :].rearrange("p u (m t) -> p t m u", t=PACK),
             )
 
         q_words = q_sb[:].bitcast(F32)
@@ -146,27 +136,23 @@ def tile_qmlp_s_kernel(
         x_words = x_grouped[:].bitcast(F32).rearrange("p (h r u) -> p h r u", h=ROW_HALVES, u=2)
         x_codes = keep.tile([P, ROWS], U32, align_bytes=64)
         x_scales = keep.tile([P, ROWS], U8, align_bytes=64)
-        for half in range(ROW_HALVES):
-            window = q_words[:, half * WINDOW_WORDS : (half + 1) * WINDOW_WORDS]
-            transposed = transpose_windows(nc, psum_t, identity[:], [window])
-            leave_psum(half, x_words[:, half, :, :], transposed[:, 0, :, :].rearrange("p u r -> p r u"))
-        for t in range(PACK):
-            cols = slice(t * P, (t + 1) * P)
-            nc.vector.quantize_mx(
-                out=w1_codes[:, cols].bitcast(FP8X4),
-                scales=w1_scales[:, cols],
-                in_=w1_grouped[:, t * P * PACK : (t + 1) * P * PACK],
-            )
-        nc.vector.quantize_mx(out=x_codes[:].bitcast(FP8X4), scales=x_scales[:], in_=x_grouped[:])
+        q_t = {}
 
-        complete_first_array(nc, w2_slots[0])
+        def transpose_q(half):
+            window = q_words[:, half * WINDOW_WORDS : (half + 1) * WINDOW_WORDS]
+            q_t[half] = transpose_windows(nc, psum_t, identity[:], [window])
+
+        def leave_q(half, engine):
+            leave_psum(engine, x_words[:, half, :, :], q_t[half][:, 0, :, :].rearrange("p u r -> p r u"))
 
         h_planes = keep.tile([P, PACK, ROWS], BF16)
-        for t in range(PACK):
+        hidden = {}
+
+        def layer_1(t):
             cols = slice(t * P, (t + 1) * P)
-            hidden = psum_mx.tile([P, ROWS], F32, tag="mx")
+            hidden[t] = psum_mx.tile([P, ROWS], F32, tag="mx", name="hidden")
             nc.tensor.matmul_mx(
-                out=hidden[:],
+                out=hidden[t][:],
                 lhsT=w1_codes[:, cols].bitcast(FP8X4),
                 lhsT_scale=w1_scales[:, cols],
                 rhs=x_codes[:].bitcast(FP8X4),
@@ -174,11 +160,13 @@ def tile_qmlp_s_kernel(
                 start=True,
                 stop=True,
             )
-            if t % 2 == 0:
-                nc.scalar.activation(out=h_planes[:, t, :], in_=hidden[:], func=ACT.Relu, bias=b1_sb[:, t : t + 1])
+
+        def relu(t, engine):
+            if engine == "S":
+                nc.scalar.activation(out=h_planes[:, t, :], in_=hidden[t][:], func=ACT.Relu, bias=b1_sb[:, t : t + 1])
             else:
                 nc.vector.tensor_scalar(
-                    out=h_planes[:, t, :], in0=hidden[:], scalar1=b1_sb[:, t : t + 1], scalar2=0.0,
+                    out=h_planes[:, t, :], in0=hidden[t][:], scalar1=b1_sb[:, t : t + 1], scalar2=0.0,
                     op0=ALU.add, op1=ALU.max,
                 )
 
@@ -197,14 +185,18 @@ def tile_qmlp_s_kernel(
         h_scales = keep.tile([P, ROWS], U8, align_bytes=64)
         b2_sb = keep.tile([P, COLUMNS_2], BF16)
         result = keep.tile([P, CHUNKS, ROW_HALVES, CHUNK], F32)
+        w2_t = {}
         products = {}
 
         def transpose_w2(chunk):
             first = chunk * (CHUNK // P)
-            last = first + CHUNK // P
-            transposed = transpose_windows(nc, psum_t, identity[:], windows[first:last])
+            w2_t[chunk] = transpose_windows(nc, psum_t, identity[:], windows[first : first + CHUNK // P])
+
+        def leave_w2(chunk):
+            first = chunk * (CHUNK // P)
             nc.scalar.copy(
-                out=w2_grouped_words[:, first:last, :, :], in_=transposed[:].rearrange("p n u o -> p n o u")
+                out=w2_grouped_words[:, first : first + CHUNK // P, :, :],
+                in_=w2_t[chunk][:].rearrange("p n u o -> p n o u"),
             )
 
         def quantise_w2(chunk):
@@ -215,13 +207,42 @@ def tile_qmlp_s_kernel(
                 in_=w2_grouped[:, chunk * CHUNK * PACK : (chunk + 1) * CHUNK * PACK],
             )
 
-        def multiply(chunk):
+        def spread_b2():
+            for first in range(0, COLUMNS_2, 2 * BANK):
+                width = min(2 * BANK, COLUMNS_2 - first)
+                spread = psum_mx.tile([P, width], BF16, tag="mx", name="spread")
+                for start in range(0, width, BANK):
+                    nc.tensor.matmul(
+                        out=spread[:, start : start + BANK],
+                        lhsT=ones[:],
+                        rhs=b2_rows[:, first + start : first + start + BANK],
+                        start=True,
+                        stop=True,
+                    )
+                nc.scalar.copy(out=b2_sb[:, first : first + width], in_=spread[:])
+
+        def interleave_h(half):
+            nc.vector.tensor_scalar_mul(
+                out=h_grouped[:, half * P * PACK : (half + 1) * P * PACK].rearrange("p (r t) -> p r t", t=PACK),
+                in0=h_planes[:, :, half * P : (half + 1) * P].rearrange("p t r -> p r t"),
+                scalar1=sign[:, 0:1],
+            )
+
+        def quantise_h(half):
+            rows = slice(half * P, (half + 1) * P)
+            nc.vector.quantize_mx(
+                out=h_codes[:, rows].bitcast(FP8X4),
+                scales=h_scales[:, rows],
+                in_=h_grouped[:, half * P * PACK : (half + 1) * P * PACK],
+            )
+
+        def layer_2(chunk):
             cols = slice(chunk * CHUNK, (chunk + 1) * CHUNK)
-            product = psum_mx.tile([P, ROW_HALVES, CHUNK], F32, tag="mx")
+            products[chunk] = psum_mx.tile([P, ROW_HALVES, CHUNK], F32, tag="mx", name="product")
             for half in range(ROW_HALVES):
                 rows = slice(half * P, (half + 1) * P)
                 nc.tensor.matmul_mx(
-                    out=product[:, half, :],
+                    out=products[chunk][:, half, :],
                     lhsT=h_codes[:, rows].bitcast(FP8X4),
                     lhsT_scale=h_scales[:, rows],
                     rhs=w2_codes[:, cols].bitcast(FP8X4),
@@ -229,16 +250,8 @@ def tile_qmlp_s_kernel(
                     start=True,
                     stop=True,
                 )
-            products[chunk] = product
 
-        def add_bias_and_store(chunk):
-            cols = slice(chunk * CHUNK, (chunk + 1) * CHUNK)
-            nc.vector.tensor_tensor(
-                out=result[:, chunk, :, :],
-                in0=products[chunk][:],
-                in1=b2_sb[:, cols].unsqueeze(1).to_broadcast([P, ROW_HALVES, CHUNK]),
-                op=ALU.add,
-            )
+        def store(chunk):
             for n, c in enumerate(ORDER):
                 low = max(chunk * CHUNK, n * D_OUT)
                 high = min((chunk + 1) * CHUNK, (n + 1) * D_OUT)
@@ -248,51 +261,65 @@ def tile_qmlp_s_kernel(
                         in_=result[:, chunk, :, low - chunk * CHUNK : high - chunk * CHUNK],
                     )
 
-        for chunk in range(EARLY):
-            transpose_w2(chunk)
-
-        for first in range(0, COLUMNS_2, 2 * BANK):
-            width = min(2 * BANK, COLUMNS_2 - first)
-            spread = psum_mx.tile([P, width], BF16, tag="mx")
-            for start in range(0, width, BANK):
-                nc.tensor.matmul(
-                    out=spread[:, start : start + BANK],
-                    lhsT=ones[:],
-                    rhs=b2_rows[:, first + start : first + start + BANK],
-                    start=True,
-                    stop=True,
-                )
-            nc.scalar.copy(out=b2_sb[:, first : first + width], in_=spread[:])
-
-        for half in range(ROW_HALVES):
-            nc.vector.tensor_scalar_mul(
-                out=h_grouped[:, half * P * PACK : (half + 1) * P * PACK].rearrange("p (r t) -> p r t", t=PACK),
-                in0=h_planes[:, :, half * P : (half + 1) * P].rearrange("p t r -> p r t"),
-                scalar1=sign[:, 0:1],
+        def add_bias_and_store(chunk):
+            cols = slice(chunk * CHUNK, (chunk + 1) * CHUNK)
+            nc.vector.tensor_tensor(
+                out=result[:, chunk, :, :],
+                in0=products[chunk][:],
+                in1=b2_sb[:, cols].unsqueeze(1).to_broadcast([P, ROW_HALVES, CHUNK]),
+                op=ALU.add,
             )
+            store(chunk)
+
+        negate(w1_slots[0][:, :, 4:6, :], w1_slots[0][:, :, 0:2, :])
+        negate(w1_slots[1][:, :, 1:5:3, :], w1_slots[0][:, :, 2:4, :])
+        nc.vector.tensor_copy(out=w1_slots[1][:, :, 0, :], in_=w1_slots[0][:, :, 3, :])
+        nc.vector.tensor_copy(out=w1_slots[1][:, :, 2:4, :], in_=w1_slots[0][:, :, 1:5:3, :])
+        nc.vector.tensor_copy(out=w1_slots[1][:, :, 5, :], in_=w1_slots[0][:, :, 2, :])
+        negate(q_view[:, :, I, :], q_view[:, :, I, :])
+        for n in range(COMPONENTS):
+            transpose_w1(n)
+            leave_w1(n, "VS"[n % 2])
         for half in range(ROW_HALVES):
-            rows = slice(half * P, (half + 1) * P)
+            transpose_q(half)
+            leave_q(half, "VS"[half])
+        for t in range(PACK):
+            cols = slice(t * P, (t + 1) * P)
             nc.vector.quantize_mx(
-                out=h_codes[:, rows].bitcast(FP8X4),
-                scales=h_scales[:, rows],
-                in_=h_grouped[:, half * P * PACK : (half + 1) * P * PACK],
+                out=w1_codes[:, cols].bitcast(FP8X4),
+                scales=w1_scales[:, cols],
+                in_=w1_grouped[:, t * P * PACK : (t + 1) * P * PACK],
             )
-
-        nc.vector.tensor_scalar_mul(
-            out=w2_slots[1][:, :, 1:5:3, :], in0=w2_slots[0][:, :, 2:4, :], scalar1=-1.0
-        )
-        nc.vector.tensor_scalar_mul(out=w2_slots[1][:, :, 3, :], in0=w2_slots[0][:, :, 0, :], scalar1=-1.0)
-        transpose_w2(EARLY)
-        for chunk in range(EARLY):
-            quantise_w2(chunk)
-
-        for chunk in range(EARLY):
-            multiply(chunk)
-        for chunk in range(EARLY + 1, CHUNKS):
+        nc.vector.quantize_mx(out=x_codes[:].bitcast(FP8X4), scales=x_scales[:], in_=x_grouped[:])
+        nc.scalar.copy(out=w2_slots[1][:, :, 2, :], in_=w2_slots[0][:, :, 1, :])
+        nc.scalar.copy(out=w2_slots[1][:, :, 5, :], in_=w2_slots[0][:, :, 2, :])
+        nc.scalar.copy(out=w2_slots[1][:, :, 0, :], in_=w2_slots[0][:, :, 3, :])
+        negate(w2_slots[0][:, :, 4:6, :], w2_slots[0][:, :, 0:2, :])
+        negate(w2_slots[1][:, :, 3, :], w2_slots[0][:, :, 0, :])
+        negate(w2_slots[1][:, :, 1:5:3, :], w2_slots[0][:, :, 2:4, :])
+        for t in range(PACK):
+            layer_1(t)
+            relu(t, "SV"[t % 2])
+        for chunk in range(3):
             transpose_w2(chunk)
+            leave_w2(chunk)
+        spread_b2()
+        interleave_h(0)
+        interleave_h(1)
+        quantise_h(0)
+        quantise_h(1)
+        transpose_w2(3)
+        leave_w2(3)
+        for chunk in range(3):
+            quantise_w2(chunk)
+        for chunk in range(3):
+            layer_2(chunk)
+        for chunk in range(4, CHUNKS):
+            transpose_w2(chunk)
+            leave_w2(chunk)
         for chunk in range(CHUNKS):
-            if chunk >= EARLY:
-                multiply(chunk)
+            if chunk >= 3:
+                layer_2(chunk)
             add_bias_and_store(chunk)
-            if EARLY <= chunk + LEAD < CHUNKS:
-                quantise_w2(chunk + LEAD)
+            if 3 <= chunk + 2 < CHUNKS:
+                quantise_w2(chunk + 2)

@@ -184,27 +184,29 @@ def tile_qmlp_s_kernel(
         h_codes = keep.tile([P, ROWS], U32, align_bytes=64)
         h_scales = keep.tile([P, ROWS], U8, align_bytes=64)
         b2_sb = keep.tile([P, COLUMNS_2], BF16)
-        result = keep.tile([P, CHUNKS, ROW_HALVES, CHUNK], F32)
+        pieces = [(0, 2), (2, 2), (4, 2), (6, 2), (8, 2), (10, 1), (11, 1)]
+        results = {}
         w2_t = {}
         products = {}
 
         def transpose_w2(chunk):
-            first = chunk * (CHUNK // P)
-            w2_t[chunk] = transpose_windows(nc, psum_t, identity[:], windows[first : first + CHUNK // P])
+            first, count = pieces[chunk]
+            w2_t[chunk] = transpose_windows(nc, psum_t, identity[:], windows[first : first + count])
 
         def leave_w2(chunk):
-            first = chunk * (CHUNK // P)
+            first, count = pieces[chunk]
             nc.scalar.copy(
-                out=w2_grouped_words[:, first : first + CHUNK // P, :, :],
+                out=w2_grouped_words[:, first : first + count, :, :],
                 in_=w2_t[chunk][:].rearrange("p n u o -> p n o u"),
             )
 
         def quantise_w2(chunk):
-            cols = slice(chunk * CHUNK, (chunk + 1) * CHUNK)
+            first, count = pieces[chunk]
+            cols = slice(first * P, (first + count) * P)
             nc.vector.quantize_mx(
                 out=w2_codes[:, cols].bitcast(FP8X4),
                 scales=w2_scales[:, cols],
-                in_=w2_grouped[:, chunk * CHUNK * PACK : (chunk + 1) * CHUNK * PACK],
+                in_=w2_grouped[:, first * P * PACK : (first + count) * P * PACK],
             )
 
         def spread_b2():
@@ -237,8 +239,9 @@ def tile_qmlp_s_kernel(
             )
 
         def layer_2(chunk):
-            cols = slice(chunk * CHUNK, (chunk + 1) * CHUNK)
-            products[chunk] = psum_mx.tile([P, ROW_HALVES, CHUNK], F32, tag="mx", name="product")
+            first, count = pieces[chunk]
+            cols = slice(first * P, (first + count) * P)
+            products[chunk] = psum_mx.tile([P, ROW_HALVES, count * P], F32, tag="mx", name="product")
             for half in range(ROW_HALVES):
                 rows = slice(half * P, (half + 1) * P)
                 nc.tensor.matmul_mx(
@@ -252,21 +255,24 @@ def tile_qmlp_s_kernel(
                 )
 
         def store(chunk):
+            first, count = pieces[chunk]
             for n, c in enumerate(ORDER):
-                low = max(chunk * CHUNK, n * D_OUT)
-                high = min((chunk + 1) * CHUNK, (n + 1) * D_OUT)
+                low = max(first * P, n * D_OUT)
+                high = min((first + count) * P, (n + 1) * D_OUT)
                 if low < high:
                     nc.sync.dma_start(
                         out=outs[c].rearrange("(p h) o -> p h o", h=ROW_HALVES)[:, :, low - n * D_OUT : high - n * D_OUT],
-                        in_=result[:, chunk, :, low - chunk * CHUNK : high - chunk * CHUNK],
+                        in_=results[chunk][:, :, low - first * P : high - first * P],
                     )
 
         def add_bias_and_store(chunk):
-            cols = slice(chunk * CHUNK, (chunk + 1) * CHUNK)
+            first, count = pieces[chunk]
+            cols = slice(first * P, (first + count) * P)
+            results[chunk] = keep.tile([P, ROW_HALVES, count * P], F32, name="result%d" % chunk)
             nc.vector.tensor_tensor(
-                out=result[:, chunk, :, :],
+                out=results[chunk][:],
                 in0=products[chunk][:],
-                in1=b2_sb[:, cols].unsqueeze(1).to_broadcast([P, ROW_HALVES, CHUNK]),
+                in1=b2_sb[:, cols].unsqueeze(1).to_broadcast([P, ROW_HALVES, count * P]),
                 op=ALU.add,
             )
             store(chunk)
@@ -314,12 +320,21 @@ def tile_qmlp_s_kernel(
             quantise_w2(chunk)
         for chunk in range(3):
             layer_2(chunk)
-        for chunk in range(4, CHUNKS):
+        for chunk in range(4, len(pieces)):
             transpose_w2(chunk)
             leave_w2(chunk)
-        for chunk in range(CHUNKS):
-            if chunk >= 3:
-                layer_2(chunk)
-            add_bias_and_store(chunk)
-            if 3 <= chunk + 2 < CHUNKS:
-                quantise_w2(chunk + 2)
+        add_bias_and_store(0)
+        add_bias_and_store(1)
+        quantise_w2(3)
+        add_bias_and_store(2)
+        quantise_w2(4)
+        layer_2(3)
+        add_bias_and_store(3)
+        quantise_w2(5)
+        quantise_w2(6)
+        layer_2(4)
+        add_bias_and_store(4)
+        layer_2(5)
+        layer_2(6)
+        add_bias_and_store(5)
+        add_bias_and_store(6)

import concourse.mybir as mybir
from concourse.masks import make_identity

F32 = mybir.dt.float32
BF16 = mybir.dt.bfloat16
U32 = mybir.dt.uint32
U8 = mybir.dt.uint8
FP8X4 = mybir.dt.float8_e4m3fn_x4
ALU = mybir.AluOpType
ACT = mybir.ActivationFunctionType

P = 128
PACK = 4
COMPONENTS = 4
ROWS, FEATURES, D_OUT = 256, 128, 384
ROW_HALVES = ROWS // P
WORDS = FEATURES // 2
WINDOW_WORDS = COMPONENTS * WORDS
SLOTS = 6
R, I, J, K = 0, 1, 2, 3
WINDOW = {J: (0, 0), R: (0, 2), I: (1, 0), K: (1, 2)}
RAW_SLOT = {J: 0, K: 1, R: 2, I: 3}
ORDER = (J, R, I, K)
OUT_TILES = D_OUT // P
COLUMNS_2 = COMPONENTS * D_OUT
BANK = 512
CHUNK = 256
CHUNKS = COLUMNS_2 // CHUNK
EARLY = 2 * D_OUT // CHUNK
FLOPS = 2 * ROWS * 512 * (COMPONENTS * FEATURES + COLUMNS_2)


def transpose_windows(nc, psum, identity, windows):
    transposed = psum.tile([P, len(windows), 2, P], F32, tag="transposed")
    for n, window in enumerate(windows):
        halves = window.rearrange("p (m u) -> p u m", u=2)
        for u in range(2):
            nc.tensor.transpose(transposed[:, n, u, :], halves[:, u, :], identity)
    return transposed


def tile_qmlp_s_kernel(
    tc,
    q_r, q_i, q_j, q_k,
    W1_r, W1_i, W1_j, W1_k,
    b1_r, b1_i, b1_j, b1_k,
    W2_r, W2_i, W2_j, W2_k,
    b2_r, b2_i, b2_j, b2_k,
    out_0, out_1, out_2, out_3,
):
    nc = tc.nc
    q = (q_r, q_i, q_j, q_k)
    W1 = (W1_r, W1_i, W1_j, W1_k)
    b1 = (b1_r, b1_i, b1_j, b1_k)
    W2 = (W2_r, W2_i, W2_j, W2_k)
    b2 = (b2_r, b2_i, b2_j, b2_k)
    outs = (out_0, out_1, out_2, out_3)

    with (
        tc.tile_pool(name="keep", bufs=1) as keep,
        tc.psum_pool(name="psum_t", bufs=4) as psum_t,
        tc.psum_pool(name="psum_mx", bufs=4) as psum_mx,
        tc.manual_schedule(),
    ):
        identity = keep.tile([P, P], F32)
        nc.vector.memset(identity[:], 0.0)
        make_identity(nc, identity[:], nomemset=True)
        sign = keep.tile([P, 1], F32)
        nc.vector.memset(sign[:], 1.0)
        nc.vector.memset(sign[32 * I : 32 * I + 32, :], -1.0)
        b2_rows = keep.tile([P, COLUMNS_2], BF16)
        nc.vector.memset(b2_rows[:].bitcast(mybir.dt.int32), 0)
        ones = keep.tile([P, P], BF16)
        nc.vector.memset(ones[:], 1.0)

        q_sb = keep.tile([P, ROW_HALVES * COMPONENTS * FEATURES], BF16)
        q_view = q_sb[:].rearrange("p (h c f) -> p h c f", h=ROW_HALVES, c=COMPONENTS)
        w1_first = keep.tile([P, SLOTS * FEATURES], BF16)
        w1_second = keep.tile([P, SLOTS * FEATURES], BF16)
        w1_slots = [a[:].rearrange("p (t s f) -> p t s f", t=1, s=SLOTS) for a in (w1_first, w1_second)]
        w2_first = keep.tile([P, OUT_TILES * SLOTS * FEATURES], BF16)
        w2_second = keep.tile([P, OUT_TILES * SLOTS * FEATURES], BF16)
        w2_slots = [a[:].rearrange("p (t s f) -> p t s f", t=OUT_TILES, s=SLOTS) for a in (w2_first, w2_second)]
        b1_sb = keep.tile([P, PACK], BF16)

        hardware_queues = (nc.sync, nc.scalar)
        for n, c in enumerate((J, K, R, I)):
            hardware_queues[n % 2].dma_start(out=w1_slots[0][:, 0, RAW_SLOT[c], :], in_=W1[c])
        for n, c in enumerate((I, R, J, K)):
            hardware_queues[n % 2].dma_start(
                out=q_view[:, :, c, :], in_=q[c].rearrange("(p h) f -> p h f", h=ROW_HALVES)
            )
        table_warmer = keep.tile([P, 1], F32)
        nc.scalar.activation(out=table_warmer[:], in_=sign[:], func=ACT.Relu)
        for c in (J, K, R, I):
            nc.sync.dma_start(
                out=w2_slots[0][:, :, RAW_SLOT[c], :], in_=W2[c].rearrange("(t p) f -> p t f", p=P)
            )
        for c in range(COMPONENTS):
            nc.sync.dma_start(out=b1_sb[32 * c : 32 * c + 32, :], in_=b1[c].rearrange("(m t) -> m t", t=PACK))
        for n, c in enumerate(ORDER):
            nc.sync.dma_start(out=b2_rows[0:1, n * D_OUT : (n + 1) * D_OUT], in_=b2[c].unsqueeze(0))

        def leave_psum(engine, out, in_):
            if engine == "V":
                nc.vector.tensor_copy(out=out, in_=in_)
            else:
                nc.scalar.copy(out=out, in_=in_)

        def negate(out, in_):
            nc.vector.tensor_scalar_mul(out=out, in0=in_, scalar1=-1.0)

        w1_words = [a[:].bitcast(F32) for a in (w1_first, w1_second)]
        w1_grouped = keep.tile([P, COMPONENTS * FEATURES * PACK], BF16, align_bytes=64)
        w1_grouped_words = w1_grouped[:].bitcast(F32).rearrange(
            "p (t c m u) -> p t c m u", t=PACK, c=COMPONENTS, u=2
        )
        w1_codes = keep.tile([P, COMPONENTS * FEATURES], U32, align_bytes=64)
        w1_scales = keep.tile([P, COMPONENTS * FEATURES], U8, align_bytes=64)
        w1_t = {}

        def transpose_w1(n):
            array, slot = WINDOW[ORDER[n]]
            window = w1_words[array][:, slot * WORDS : slot * WORDS + WINDOW_WORDS]
            w1_t[n] = transpose_windows(nc, psum_t, identity[:], [window])

        def leave_w1(n, engine):
            leave_psum(
                engine,
                w1_grouped_words[:, :, ORDER[n], :, :],
                w1_t[n][:, 0, :, :].rearrange("p u (m t) -> p t m u", t=PACK),
            )

        q_words = q_sb[:].bitcast(F32)
        x_grouped = keep.tile([P, ROWS * PACK], BF16, align_bytes=64)
        x_words = x_grouped[:].bitcast(F32).rearrange("p (h r u) -> p h r u", h=ROW_HALVES, u=2)
        x_codes = keep.tile([P, ROWS], U32, align_bytes=64)
        x_scales = keep.tile([P, ROWS], U8, align_bytes=64)
        q_t = {}

        def transpose_q(half):
            window = q_words[:, half * WINDOW_WORDS : (half + 1) * WINDOW_WORDS]
            q_t[half] = transpose_windows(nc, psum_t, identity[:], [window])

        def leave_q(half, engine):
            leave_psum(engine, x_words[:, half, :, :], q_t[half][:, 0, :, :].rearrange("p u r -> p r u"))

        h_planes = keep.tile([P, PACK, ROWS], BF16)
        hidden = {}

        def layer_1(t):
            cols = slice(t * P, (t + 1) * P)
            hidden[t] = psum_mx.tile([P, ROWS], F32, tag="mx", name="hidden")
            nc.tensor.matmul_mx(
                out=hidden[t][:],
                lhsT=w1_codes[:, cols].bitcast(FP8X4),
                lhsT_scale=w1_scales[:, cols],
                rhs=x_codes[:].bitcast(FP8X4),
                rhs_scale=x_scales[:],
                start=True,
                stop=True,
            )

        def relu(t, engine):
            if engine == "S":
                nc.scalar.activation(out=h_planes[:, t, :], in_=hidden[t][:], func=ACT.Relu, bias=b1_sb[:, t : t + 1])
            else:
                nc.vector.tensor_scalar(
                    out=h_planes[:, t, :], in0=hidden[t][:], scalar1=b1_sb[:, t : t + 1], scalar2=0.0,
                    op0=ALU.add, op1=ALU.max,
                )

        w2_words = [a[:].bitcast(F32).rearrange("p (t w) -> p t w", t=OUT_TILES) for a in (w2_first, w2_second)]
        windows = [
            w2_words[WINDOW[c][0]][:, tile, WINDOW[c][1] * WORDS : WINDOW[c][1] * WORDS + WINDOW_WORDS]
            for c in ORDER
            for tile in range(OUT_TILES)
        ]
        w2_grouped = keep.tile([P, COLUMNS_2 * PACK], BF16, align_bytes=64)
        w2_grouped_words = w2_grouped[:].bitcast(F32).rearrange("p (n o u) -> p n o u", o=P, u=2)
        w2_codes = keep.tile([P, COLUMNS_2], U32, align_bytes=64)
        w2_scales = keep.tile([P, COLUMNS_2], U8, align_bytes=64)
        h_grouped = keep.tile([P, ROWS * PACK], BF16, align_bytes=64)
        h_codes = keep.tile([P, ROWS], U32, align_bytes=64)
        h_scales = keep.tile([P, ROWS], U8, align_bytes=64)
        b2_sb = keep.tile([P, COLUMNS_2], BF16)
        pieces = [(0, 2), (2, 2), (4, 2), (6, 2), (8, 2), (10, 1), (11, 1)]
        results = {}
        w2_t = {}
        products = {}

        def transpose_w2(chunk):
            first, count = pieces[chunk]
            w2_t[chunk] = transpose_windows(nc, psum_t, identity[:], windows[first : first + count])

        def leave_w2(chunk):
            first, count = pieces[chunk]
            nc.scalar.copy(
                out=w2_grouped_words[:, first : first + count, :, :],
                in_=w2_t[chunk][:].rearrange("p n u o -> p n o u"),
            )

        def quantise_w2(chunk):
            first, count = pieces[chunk]
            cols = slice(first * P, (first + count) * P)
            nc.vector.quantize_mx(
                out=w2_codes[:, cols].bitcast(FP8X4),
                scales=w2_scales[:, cols],
                in_=w2_grouped[:, first * P * PACK : (first + count) * P * PACK],
            )

        def spread_b2():
            for first in range(0, COLUMNS_2, 2 * BANK):
                width = min(2 * BANK, COLUMNS_2 - first)
                spread = psum_mx.tile([P, width], BF16, tag="mx", name="spread")
                for start in range(0, width, BANK):
                    nc.tensor.matmul(
                        out=spread[:, start : start + BANK],
                        lhsT=ones[:],
                        rhs=b2_rows[:, first + start : first + start + BANK],
                        start=True,
                        stop=True,
                    )
                nc.scalar.copy(out=b2_sb[:, first : first + width], in_=spread[:])

        def interleave_h(half):
            nc.vector.tensor_scalar_mul(
                out=h_grouped[:, half * P * PACK : (half + 1) * P * PACK].rearrange("p (r t) -> p r t", t=PACK),
                in0=h_planes[:, :, half * P : (half + 1) * P].rearrange("p t r -> p r t"),
                scalar1=sign[:, 0:1],
            )

        def quantise_h(half):
            rows = slice(half * P, (half + 1) * P)
            nc.vector.quantize_mx(
                out=h_codes[:, rows].bitcast(FP8X4),
                scales=h_scales[:, rows],
                in_=h_grouped[:, half * P * PACK : (half + 1) * P * PACK],
            )

        def layer_2(chunk):
            first, count = pieces[chunk]
            cols = slice(first * P, (first + count) * P)
            products[chunk] = psum_mx.tile([P, ROW_HALVES, count * P], F32, tag="mx", name="product")
            for half in range(ROW_HALVES):
                rows = slice(half * P, (half + 1) * P)
                nc.tensor.matmul_mx(
                    out=products[chunk][:, half, :],
                    lhsT=h_codes[:, rows].bitcast(FP8X4),
                    lhsT_scale=h_scales[:, rows],
                    rhs=w2_codes[:, cols].bitcast(FP8X4),
                    rhs_scale=w2_scales[:, cols],
                    start=True,
                    stop=True,
                )

        def store(chunk):
            first, count = pieces[chunk]
            for n, c in enumerate(ORDER):
                low = max(first * P, n * D_OUT)
                high = min((first + count) * P, (n + 1) * D_OUT)
                if low < high:
                    nc.sync.dma_start(
                        out=outs[c].rearrange("(p h) o -> p h o", h=ROW_HALVES)[:, :, low - n * D_OUT : high - n * D_OUT],
                        in_=results[chunk][:, :, low - first * P : high - first * P],
                    )

        def add_bias_and_store(chunk):
            first, count = pieces[chunk]
            cols = slice(first * P, (first + count) * P)
            results[chunk] = keep.tile([P, ROW_HALVES, count * P], F32, name="result%d" % chunk)
            nc.vector.tensor_tensor(
                out=results[chunk][:],
                in0=products[chunk][:],
                in1=b2_sb[:, cols].unsqueeze(1).to_broadcast([P, ROW_HALVES, count * P]),
                op=ALU.add,
            )
            store(chunk)

        negate(w1_slots[0][:, :, 4:6, :], w1_slots[0][:, :, 0:2, :])
        negate(w1_slots[1][:, :, 1:5:3, :], w1_slots[0][:, :, 2:4, :])
        nc.vector.tensor_copy(out=w1_slots[1][:, :, 0, :], in_=w1_slots[0][:, :, 3, :])
        nc.vector.tensor_copy(out=w1_slots[1][:, :, 2:4, :], in_=w1_slots[0][:, :, 1:5:3, :])
        nc.vector.tensor_copy(out=w1_slots[1][:, :, 5, :], in_=w1_slots[0][:, :, 2, :])
        negate(q_view[:, :, I, :], q_view[:, :, I, :])
        for n in range(COMPONENTS):
            transpose_w1(n)
            leave_w1(n, "VS"[n % 2])
        for half in range(ROW_HALVES):
            transpose_q(half)
            leave_q(half, "VS"[half])
        for t in range(PACK):
            cols = slice(t * P, (t + 1) * P)
            nc.vector.quantize_mx(
                out=w1_codes[:, cols].bitcast(FP8X4),
                scales=w1_scales[:, cols],
                in_=w1_grouped[:, t * P * PACK : (t + 1) * P * PACK],
            )
        nc.vector.quantize_mx(out=x_codes[:].bitcast(FP8X4), scales=x_scales[:], in_=x_grouped[:])
        nc.scalar.copy(out=w2_slots[1][:, :, 2, :], in_=w2_slots[0][:, :, 1, :])
        nc.scalar.copy(out=w2_slots[1][:, :, 5, :], in_=w2_slots[0][:, :, 2, :])
        nc.scalar.copy(out=w2_slots[1][:, :, 0, :], in_=w2_slots[0][:, :, 3, :])
        negate(w2_slots[0][:, :, 4:6, :], w2_slots[0][:, :, 0:2, :])
        negate(w2_slots[1][:, :, 3, :], w2_slots[0][:, :, 0, :])
        negate(w2_slots[1][:, :, 1:5:3, :], w2_slots[0][:, :, 2:4, :])
        for t in range(PACK):
            layer_1(t)
            relu(t, "SV"[t % 2])
        for chunk in range(3):
            transpose_w2(chunk)
            leave_w2(chunk)
        spread_b2()
        interleave_h(0)
        interleave_h(1)
        quantise_h(0)
        quantise_h(1)
        transpose_w2(3)
        leave_w2(3)
        for chunk in range(3):
            quantise_w2(chunk)
        for chunk in range(3):
            layer_2(chunk)
        for chunk in range(4, len(pieces)):
            transpose_w2(chunk)
            leave_w2(chunk)
        add_bias_and_store(0)
        add_bias_and_store(1)
        quantise_w2(3)
        add_bias_and_store(2)
        quantise_w2(4)
        layer_2(3)
        add_bias_and_store(3)
        quantise_w2(5)
        quantise_w2(6)
        layer_2(4)
        add_bias_and_store(4)
        layer_2(5)
        layer_2(6)
        add_bias_and_store(5)
        add_bias_and_store(6)
